import numpy as np
import ml_dtypes


def mxq(x, axis, fmt="e4m3"):
    dtype, down = {"e4m3": (ml_dtypes.float8_e4m3fn, 7), "e5m2": (ml_dtypes.float8_e5m2, 14)}[fmt]
    v = np.moveaxis(np.asarray(x, np.float32).astype(ml_dtypes.bfloat16).astype(np.float64), axis, -1)
    blocks = v.reshape(v.shape[:-1] + (-1, 32))
    amax = np.abs(blocks).max(-1, keepdims=True)
    byte = np.maximum(np.where(amax > 0, np.frexp(amax)[1] - 1 + 127, 0) - down, 1)
    scale = np.exp2(byte - 127.0)
    codes = (blocks / scale).astype(np.float32).astype(dtype).astype(np.float64)
    return np.moveaxis((codes * scale).reshape(v.shape), -1, axis)


WIDE = False


def mx_kscale(k):
    if not WIDE:
        return np.ones(k)
    levels = np.array([10, -10, 5, -5, 0])
    a = np.random.permutation(np.resize(levels, k // 512 * 4)).reshape(k // 512, 4)
    idx = np.arange(k)
    return np.exp2(a[idx // 512, idx % 128 // 32])


BF16 = ml_dtypes.bfloat16


def bf(x):
    return np.asarray(x, np.float32).astype(BF16)


def f64(x):
    return np.asarray(x).astype(np.float64)


B, N, NF, ND, NH = 1, 128, 128, 512, 512


def setup_inputs():
    s = mx_kscale(ND)
    t = mx_kscale(NH)
    return {
        "atom_features": bf(np.random.standard_normal((B, N, NF))),
        "distance_matrix": bf(np.random.random((B, N, N, ND)) * s),
        "distance_matrix_mask": bf(0.25 + 0.75 * np.random.random((B, N, N))),
        "W_cf": bf(np.random.standard_normal((NF, NH)) / np.sqrt(NF) * t),
        "W_df": bf(np.random.standard_normal((ND, NH)) * 1.5 / np.sqrt(ND) / s[:, None]),
        "W_fc": bf(np.random.standard_normal((NH, NF)) / np.sqrt(NH) / t[:, None]),
        "b_cf": bf(np.random.standard_normal(NH) * 0.3 * t),
        "b_df": bf(np.random.standard_normal(NH) * 0.3),
    }


def reference(atom_features, distance_matrix, distance_matrix_mask, W_cf, W_df, W_fc, b_cf, b_df):
    a = f64(atom_features)
    dist_h = (mxq(f64(distance_matrix), 3, "e4m3") @ mxq(f64(W_df), 0, "e4m3")) + f64(b_df)
    atom_h = a @ f64(W_cf) + f64(b_cf)
    gated = dist_h * atom_h[:, None, :, :]
    out = mxq(gated, 3, "e4m3") @ mxq(f64(W_fc), 0, "e4m3")
    out = out * f64(distance_matrix_mask)[..., None]
    return np.tanh(out).sum(axis=2) + a

@@ -1,0 +1,207 @@
+from contextlib import ExitStack
+
+import concourse.mybir as mybir
+from concourse.masks import make_identity
+
+F32 = mybir.dt.float32
+BF16 = mybir.dt.bfloat16
+U32 = mybir.dt.uint32
+U8 = mybir.dt.uint8
+FP8X4 = mybir.dt.float8_e4m3fn_x4
+ALU = mybir.AluOpType
+ACT = mybir.ActivationFunctionType
+
+P = 128
+NA = 128
+ND = 512
+NH = 512
+NF = 128
+QJ = 4
+NQ = NA // QJ
+CHJ = 4
+FLOPS = 2 * NA * NA * ND * NH + 2 * NA * NA * NH * NF + 2 * NA * NF * NH
+
+SC_CHUNKS = ((0, 1), (0, 1, 2))
+
+
+def tile_dtnnstep_pa_t_kernel(tc, atom_features, distance_matrix, distance_matrix_mask,
+                                         W_cf, W_df, W_fc, b_cf, b_df, out):
+    nc = tc.nc
+    a_dram = atom_features.rearrange("b j f -> (b j) f")
+    d_dram = distance_matrix.rearrange("b i j k -> (b i) (j k)")
+    m_dram = distance_matrix_mask.rearrange("b i j -> (b i) j")
+    o_dram = out.rearrange("b i f -> (b i) f")
+
+    with ExitStack() as ctx:
+        const = ctx.enter_context(tc.tile_pool(name="const", bufs=1))
+        dpool = ctx.enter_context(tc.tile_pool(name="dpool", bufs=6))
+        work = ctx.enter_context(tc.tile_pool(name="work", bufs=3))
+        ps_t = ctx.enter_context(tc.psum_pool(name="ps_t", bufs=2))
+        ps_1 = ctx.enter_context(tc.psum_pool(name="ps_1", bufs=3))
+        ps_2 = ctx.enter_context(tc.psum_pool(name="ps_2", bufs=2))
+        ps_a = ctx.enter_context(tc.psum_pool(name="ps_a", bufs=1))
+
+        w_raw = const.tile([P, 4, NH], BF16, name="w_raw")
+        for u in range(2):
+            nc.sync.dma_start(out=w_raw[:, 2 * u:2 * u + 2, :],
+                                in_=W_df[256 * u:256 * u + 256, :].rearrange("(q e) h -> q e h", e=2))
+        dtiles = {}
+
+        def load(ch):
+            dt_ = dpool.tile([P, CHJ * ND], BF16, name="dt_", tag="dt_")
+            nc.sync.dma_start(out=dt_[:], in_=d_dram[:, ch * CHJ * ND:(ch + 1) * CHJ * ND])
+            dtiles[ch] = dt_
+
+        load(0)
+        a_bf = const.tile([P, NF], BF16, name="a_bf")
+        nc.scalar.dma_start(out=a_bf[:], in_=a_dram)
+        wcf_raw = const.tile([P, NH], BF16, name="wcf_raw")
+        nc.scalar.dma_start(out=wcf_raw[:], in_=W_cf)
+        bcf_bf = const.tile([P, 4], BF16, name="bcf_bf")
+        nc.scalar.dma_start(out=bcf_bf[:], in_=b_cf.rearrange("(m c) -> m c", c=4))
+        bdf_bf = const.tile([P, 4], BF16, name="bdf_bf")
+        nc.scalar.dma_start(out=bdf_bf[:], in_=b_df.rearrange("(m c) -> m c", c=4))
+        f_raw = const.tile([P, 4, NF], BF16, name="f_raw")
+        nc.scalar.dma_start(out=f_raw[:], in_=W_fc.rearrange("(p t) f -> p t f", t=4))
+        m_bf = const.tile([P, NA], BF16, name="m_bf")
+        nc.scalar.dma_start(out=m_bf[:], in_=m_dram)
+
+        ident = const.tile([P, P], F32, name="ident")
+        make_identity(nc, ident[:])
+
+        w_grp = const.tile([P, 4, P, 4], BF16, name="w_grp", align_bytes=64)
+        w_codes = const.tile([P, NH], U32, name="w_codes", align_bytes=64)
+        w_scales = const.tile([P, NH], U8, name="w_scales", align_bytes=64)
+        w_view = w_raw[:].rearrange("q t (m c) -> q c m t", c=4)
+        for c in range(2):
+            nc.vector.tensor_copy(out=w_grp[:, c], in_=w_view[:, c])
+            nc.scalar.copy(out=w_grp[:, c + 2], in_=w_view[:, c + 2])
+        for c in range(4):
+            nc.vector.quantize_mx(out=w_codes[:, c * P:(c + 1) * P].bitcast(FP8X4),
+                                  scales=w_scales[:, c * P:(c + 1) * P],
+                                  in_=w_grp[:, c].rearrange("q m t -> q (m t)"))
+        a32 = const.tile([P, NF], F32, name="a32")
+        nc.gpsimd.tensor_copy(out=a32[:], in_=a_bf[:])
+        bcf = const.tile([P, 4], F32, name="bcf")
+        nc.gpsimd.tensor_copy(out=bcf[:], in_=bcf_bf[:])
+        bdf = const.tile([P, 4], F32, name="bdf")
+        nc.gpsimd.tensor_copy(out=bdf[:], in_=bdf_bf[:])
+        wcf = const.tile([P, 4, P], BF16, name="wcf")
+        nc.scalar.copy(out=wcf[:], in_=wcf_raw[:].rearrange("f (m c) -> f c m", c=4))
+        aT_ps = ps_t.tile([P, P], F32, name="aT_ps", tag="tp")
+        nc.tensor.transpose(aT_ps[:], a32[:], ident[:])
+        aT = const.tile([P, NA], BF16, name="aT")
+        nc.scalar.copy(out=aT[:], in_=aT_ps[:])
+        at_ps = ps_t.tile([P, 4, NA], F32, name="at_ps", tag="tp")
+        for c in range(4):
+            nc.tensor.matmul(at_ps[:, c, :], lhsT=wcf[:, c, :], rhs=aT[:], start=True, stop=True)
+        gate = const.tile([P, 4, NA], F32, name="gate")
+        gbias = const.tile([P, 4, NA], F32, name="gbias")
+        for c in range(4):
+            nc.scalar.activation(out=gate[:, c, :], in_=at_ps[:, c, :], func=ACT.Identity, bias=bcf[:, c:c + 1])
+            nc.scalar.activation(out=gbias[:, c, :], in_=gate[:, c, :], func=ACT.Copy, scale=bdf[:, c:c + 1])
+
+        accT = ps_a.tile([P, NA], F32, name="accT")
+        nc.tensor.matmul(accT[:], lhsT=a32[:], rhs=ident[:], start=True, stop=False, is_transpose=True)
+
+        f_grp = const.tile([P, NF, 4], BF16, name="f_grp", align_bytes=64)
+        nc.gpsimd.tensor_scalar(out=f_grp[:], in0=f_raw[:].rearrange("p t f -> p f t"), scalar1=1.0, scalar2=0.0,
+                                op0=ALU.mult, op1=ALU.add)
+        mask = const.tile([P, NA], F32, name="mask")
+        nc.gpsimd.tensor_scalar(out=mask[:], in0=m_bf[:], scalar1=1.0, scalar2=0.0, op0=ALU.mult, op1=ALU.add)
+        f_codes = const.tile([P, NF], U32, name="f_codes", align_bytes=64)
+        f_scales = const.tile([P, NF], U8, name="f_scales", align_bytes=64)
+        nc.vector.quantize_mx(out=f_codes[:].bitcast(FP8X4), scales=f_scales[:],
+                              in_=f_grp[:].rearrange("p f t -> p (f t)"))
+
+        st = {}
+
+        def stage_a(q):
+            ch, off = divmod(q * QJ, CHJ)
+            if off == 0 and ch + 1 < NA // CHJ:
+                load(ch + 1)
+            d32 = dtiles[ch][:].bitcast(F32)
+            d_grp = work.tile([P, QJ * NA * 4], BF16, name="d_grp", tag="d_grp", align_bytes=64)
+            g32 = d_grp[:].bitcast(F32).rearrange("p (h a i u) -> p h a i u", h=2, a=2, u=2)
+            for h in range(2):
+                tp = ps_t.tile([P, 2, 2, NA], F32, name="tp", tag="tp")
+                for a in range(2):
+                    jj = off + 2 * h + a
+                    for u in range(2):
+                        nc.tensor.transpose(tp[:, a, u, :], d32[:, jj * 256 + u * P:jj * 256 + (u + 1) * P],
+                                            ident[:])
+                nc.scalar.copy(out=g32[:, h], in_=tp[:].rearrange("p a u i -> p a i u"))
+            d_codes = work.tile([P, QJ * NA], U32, name="d_codes", tag="d_codes", align_bytes=64)
+            d_scales = work.tile([P, QJ * NA], U8, name="d_scales", tag="d_scales", align_bytes=64)
+            nc.vector.quantize_mx(out=d_codes[:].bitcast(FP8X4), scales=d_scales[:], in_=d_grp[:])
+            st[("d", q)] = (d_codes, d_scales)
+
+        def stage_b(q):
+            d_codes, d_scales = st[("d", q)]
+            planes = work.tile([P, 4, QJ * NA], BF16, name="planes", tag="planes")
+            j0 = q * QJ
+            for c in range(4):
+                p1 = ps_1.tile([P, QJ * NA], F32, name="p1", tag="p1")
+                nc.tensor.matmul_mx(out=p1[:], lhsT=w_codes[:, c * P:(c + 1) * P].bitcast(FP8X4),
+                                    lhsT_scale=w_scales[:, c * P:(c + 1) * P],
+                                    rhs=d_codes[:].bitcast(FP8X4), rhs_scale=d_scales[:],
+                                    start=True, stop=True)
+                if c in SC_CHUNKS[q % 2]:
+                    for a in range(QJ):
+                        nc.scalar.activation(out=planes[:, c, a * NA:(a + 1) * NA], in_=p1[:, a * NA:(a + 1) * NA],
+                                             func=ACT.Identity, scale=gate[:, c, j0 + a:j0 + a + 1],
+                                             bias=gbias[:, c, j0 + a:j0 + a + 1])
+                else:
+                    nc.vector.scalar_tensor_tensor(
+                        out=planes[:, c, :].rearrange("p (a i) -> p a i", a=QJ),
+                        in0=p1[:].rearrange("p (a i) -> p a i", a=QJ),
+                        scalar=bdf[:, c:c + 1],
+                        in1=gate[:, c, j0:j0 + QJ].unsqueeze(2).to_broadcast([P, QJ, NA]),
+                        op0=ALU.add, op1=ALU.mult)
+            st[("p", q)] = planes
+
+        def stage_c(q):
+            planes = st[("p", q)]
+            g_grp = work.tile([P, QJ * NA, 4], BF16, name="g_grp", tag="g_grp", align_bytes=64)
+            nc.vector.tensor_copy(out=g_grp[:].rearrange("p (x y) t -> p x t y", y=4),
+                                  in_=planes[:].rearrange("p t (x y) -> p x t y", y=4))
+            g_codes = work.tile([P, QJ * NA], U32, name="g_codes", tag="g_codes", align_bytes=64)
+            g_scales = work.tile([P, QJ * NA], U8, name="g_scales", tag="g_scales", align_bytes=64)
+            nc.vector.quantize_mx(out=g_codes[:].bitcast(FP8X4), scales=g_scales[:],
+                                  in_=g_grp[:].rearrange("p w t -> p (w t)"))
+            st[("g", q)] = (g_codes, g_scales)
+
+        def stage_d(q):
+            g_codes, g_scales = st[("g", q)]
+            j0 = q * QJ
+            p2 = ps_2.tile([P, QJ, NF], F32, name="p2", tag="p2")
+            th = work.tile([P, QJ, NF], F32, name="th", tag="th")
+            for a in range(QJ):
+                nc.tensor.matmul_mx(out=p2[:, a, :], lhsT=g_codes[:, a * NA:(a + 1) * NA].bitcast(FP8X4),
+                                    lhsT_scale=g_scales[:, a * NA:(a + 1) * NA],
+                                    rhs=f_codes[:].bitcast(FP8X4), rhs_scale=f_scales[:],
+                                    start=True, stop=True)
+            for a in range(QJ):
+                nc.scalar.activation(out=th[:, a, :], in_=p2[:, a, :], func=ACT.Tanh,
+                                     scale=mask[:, j0 + a:j0 + a + 1])
+            for a in range(QJ):
+                nc.tensor.matmul(accT[:], lhsT=th[:, a, :], rhs=ident[:], start=False,
+                                 stop=(q == NQ - 1 and a == QJ - 1), is_transpose=True)
+
+        for s in range(NQ + 3):
+            if s < NQ:
+                stage_a(s)
+            if 0 <= s - 1 < NQ:
+                stage_b(s - 1)
+            if 0 <= s - 2 < NQ:
+                stage_c(s - 2)
+            if 0 <= s - 3 < NQ:
+                stage_d(s - 3)
+
+        sumT = const.tile([P, NA], F32, name="sumT")
+        nc.vector.tensor_copy(out=sumT[:], in_=accT[:])
+        res_ps = ps_t.tile([P, NF], F32, name="res_ps", tag="tp")
+        nc.tensor.transpose(res_ps[:], sumT[:], ident[:])
+        res = const.tile([P, NF], F32, name="res")
+        nc.vector.tensor_copy(out=res[:], in_=res_ps[:])
+        nc.sync.dma_start(out=o_dram, in_=res[:])

@@ -21,7 +21,7 @@ NQ = NA // QJ
 CHJ = 4
 FLOPS = 2 * NA * NA * ND * NH + 2 * NA * NA * NH * NF + 2 * NA * NF * NH
 
-SC_CHUNKS = ((0, 1), (0, 1, 2))
+SC_CHUNKS = ((0, 1), (0, 1))
 
 
 def tile_dtnnstep_pa_t_kernel(tc, atom_features, distance_matrix, distance_matrix_mask,

@@ -18,10 +18,15 @@ NH = 512
 NF = 128
 QJ = 4
 NQ = NA // QJ
-CHJ = 4
+W = QJ * NA
+LOADS_AHEAD = 6
 FLOPS = 2 * NA * NA * ND * NH + 2 * NA * NA * NH * NF + 2 * NA * NF * NH
 
-SC_CHUNKS = ((0, 1), (0, 1))
+PASSES = (
+    ((3, "v"), (0, "s"), (1, "s"), (2, "v")),
+    ((3, "v"), (0, "s"), (1, "s"), (2, "v")),
+    ((3, "v"), (0, "s"), (1, "s"), (2, "s")),
+)
 
 
 def tile_dtnnstep_pa_t_kernel(tc, atom_features, distance_matrix, distance_matrix_mask,
@@ -34,25 +39,27 @@ def tile_dtnnstep_pa_t_kernel(tc, atom_features, distance_matrix, distance_matri
 
     with ExitStack() as ctx:
         const = ctx.enter_context(tc.tile_pool(name="const", bufs=1))
-        dpool = ctx.enter_context(tc.tile_pool(name="dpool", bufs=6))
+        dpool = ctx.enter_context(tc.tile_pool(name="dpool", bufs=LOADS_AHEAD))
         work = ctx.enter_context(tc.tile_pool(name="work", bufs=3))
         ps_t = ctx.enter_context(tc.psum_pool(name="ps_t", bufs=2))
-        ps_1 = ctx.enter_context(tc.psum_pool(name="ps_1", bufs=3))
-        ps_2 = ctx.enter_context(tc.psum_pool(name="ps_2", bufs=2))
+        ps_1 = ctx.enter_context(tc.psum_pool(name="ps_1", bufs=4))
+        ps_2 = ctx.enter_context(tc.psum_pool(name="ps_2", bufs=1))
         ps_a = ctx.enter_context(tc.psum_pool(name="ps_a", bufs=1))
+        ctx.enter_context(tc.manual_schedule())
 
         w_raw = const.tile([P, 4, NH], BF16, name="w_raw")
         for u in range(2):
             nc.sync.dma_start(out=w_raw[:, 2 * u:2 * u + 2, :],
-                                in_=W_df[256 * u:256 * u + 256, :].rearrange("(q e) h -> q e h", e=2))
+                              in_=W_df[256 * u:256 * u + 256, :].rearrange("(q e) h -> q e h", e=2))
         dtiles = {}
 
-        def load(ch):
-            dt_ = dpool.tile([P, CHJ * ND], BF16, name="dt_", tag="dt_")
-            nc.sync.dma_start(out=dt_[:], in_=d_dram[:, ch * CHJ * ND:(ch + 1) * CHJ * ND])
-            dtiles[ch] = dt_
+        def load(q):
+            dt_ = dpool.tile([P, QJ * ND], BF16, name="dt_", tag="dt_")
+            nc.sync.dma_start(out=dt_[:], in_=d_dram[:, q * QJ * ND:(q + 1) * QJ * ND])
+            dtiles[q] = dt_
 
-        load(0)
+        for q in range(LOADS_AHEAD):
+            load(q)
         a_bf = const.tile([P, NF], BF16, name="a_bf")
         nc.scalar.dma_start(out=a_bf[:], in_=a_dram)
         wcf_raw = const.tile([P, NH], BF16, name="wcf_raw")
@@ -68,135 +75,190 @@ def tile_dtnnstep_pa_t_kernel(tc, atom_features, distance_matrix, distance_matri
 
         ident = const.tile([P, P], F32, name="ident")
         make_identity(nc, ident[:])
-
-        w_grp = const.tile([P, 4, P, 4], BF16, name="w_grp", align_bytes=64)
-        w_codes = const.tile([P, NH], U32, name="w_codes", align_bytes=64)
-        w_scales = const.tile([P, NH], U8, name="w_scales", align_bytes=64)
-        w_view = w_raw[:].rearrange("q t (m c) -> q c m t", c=4)
-        for c in range(2):
-            nc.vector.tensor_copy(out=w_grp[:, c], in_=w_view[:, c])
-            nc.scalar.copy(out=w_grp[:, c + 2], in_=w_view[:, c + 2])
-        for c in range(4):
-            nc.vector.quantize_mx(out=w_codes[:, c * P:(c + 1) * P].bitcast(FP8X4),
-                                  scales=w_scales[:, c * P:(c + 1) * P],
-                                  in_=w_grp[:, c].rearrange("q m t -> q (m t)"))
         a32 = const.tile([P, NF], F32, name="a32")
         nc.gpsimd.tensor_copy(out=a32[:], in_=a_bf[:])
         bcf = const.tile([P, 4], F32, name="bcf")
         nc.gpsimd.tensor_copy(out=bcf[:], in_=bcf_bf[:])
         bdf = const.tile([P, 4], F32, name="bdf")
         nc.gpsimd.tensor_copy(out=bdf[:], in_=bdf_bf[:])
+        f_grp = const.tile([P, NF, 4], BF16, name="f_grp", align_bytes=64)
+        nc.gpsimd.tensor_scalar(out=f_grp[:], in0=f_raw[:].rearrange("p t f -> p f t"), scalar1=1.0, scalar2=0.0,
+                                op0=ALU.mult, op1=ALU.add)
+        mask = const.tile([P, NA], F32, name="mask")
+        nc.gpsimd.tensor_scalar(out=mask[:], in0=m_bf[:], scalar1=1.0, scalar2=0.0, op0=ALU.mult, op1=ALU.add)
+
         wcf = const.tile([P, 4, P], BF16, name="wcf")
         nc.scalar.copy(out=wcf[:], in_=wcf_raw[:].rearrange("f (m c) -> f c m", c=4))
         aT_ps = ps_t.tile([P, P], F32, name="aT_ps", tag="tp")
         nc.tensor.transpose(aT_ps[:], a32[:], ident[:])
         aT = const.tile([P, NA], BF16, name="aT")
         nc.scalar.copy(out=aT[:], in_=aT_ps[:])
-        at_ps = ps_t.tile([P, 4, NA], F32, name="at_ps", tag="tp")
+        at_ps = ps_1.tile([P, 4, NA], F32, name="at_ps", tag="p1")
         for c in range(4):
             nc.tensor.matmul(at_ps[:, c, :], lhsT=wcf[:, c, :], rhs=aT[:], start=True, stop=True)
-        gate = const.tile([P, 4, NA], F32, name="gate")
-        gbias = const.tile([P, 4, NA], F32, name="gbias")
-        for c in range(4):
-            nc.scalar.activation(out=gate[:, c, :], in_=at_ps[:, c, :], func=ACT.Identity, bias=bcf[:, c:c + 1])
-            nc.scalar.activation(out=gbias[:, c, :], in_=gate[:, c, :], func=ACT.Copy, scale=bdf[:, c:c + 1])
-
         accT = ps_a.tile([P, NA], F32, name="accT")
         nc.tensor.matmul(accT[:], lhsT=a32[:], rhs=ident[:], start=True, stop=False, is_transpose=True)
 
-        f_grp = const.tile([P, NF, 4], BF16, name="f_grp", align_bytes=64)
-        nc.gpsimd.tensor_scalar(out=f_grp[:], in0=f_raw[:].rearrange("p t f -> p f t"), scalar1=1.0, scalar2=0.0,
-                                op0=ALU.mult, op1=ALU.add)
-        mask = const.tile([P, NA], F32, name="mask")
-        nc.gpsimd.tensor_scalar(out=mask[:], in0=m_bf[:], scalar1=1.0, scalar2=0.0, op0=ALU.mult, op1=ALU.add)
+        w_grp = const.tile([P, 4, P, 4], BF16, name="w_grp", align_bytes=64)
+        w_codes = const.tile([P, NH], U32, name="w_codes", align_bytes=64)
+        w_scales = const.tile([P, NH], U8, name="w_scales", align_bytes=64)
+        w_view = w_raw[:].rearrange("q t (m c) -> q c m t", c=4)
+        for c in (3, 0):
+            nc.vector.tensor_copy(out=w_grp[:, c], in_=w_view[:, c])
+        for c in (1, 2):
+            nc.scalar.copy(out=w_grp[:, c], in_=w_view[:, c])
+        for c in (3, 0, 1, 2):
+            nc.vector.quantize_mx(out=w_codes[:, c * P:(c + 1) * P].bitcast(FP8X4),
+                                  scales=w_scales[:, c * P:(c + 1) * P],
+                                  in_=w_grp[:, c].rearrange("q m t -> q (m t)"))
+        gate = const.tile([P, 4, NA], F32, name="gate")
+        gbias = const.tile([P, 4, NA], F32, name="gbias")
+        for c in range(4):
+            nc.vector.tensor_scalar(out=gate[:, c, :], in0=at_ps[:, c, :], scalar1=bcf[:, c:c + 1],
+                                    scalar2=None, op0=ALU.add)
         f_codes = const.tile([P, NF], U32, name="f_codes", align_bytes=64)
         f_scales = const.tile([P, NF], U8, name="f_scales", align_bytes=64)
-        nc.vector.quantize_mx(out=f_codes[:].bitcast(FP8X4), scales=f_scales[:],
-                              in_=f_grp[:].rearrange("p f t -> p (f t)"))
 
         st = {}
 
-        def stage_a(q):
-            ch, off = divmod(q * QJ, CHJ)
-            if off == 0 and ch + 1 < NA // CHJ:
-                load(ch + 1)
-            d32 = dtiles[ch][:].bitcast(F32)
-            d_grp = work.tile([P, QJ * NA * 4], BF16, name="d_grp", tag="d_grp", align_bytes=64)
-            g32 = d_grp[:].bitcast(F32).rearrange("p (h a i u) -> p h a i u", h=2, a=2, u=2)
+        def transposes(q):
+            d32 = dtiles[q][:].bitcast(F32)
+            tps = []
             for h in range(2):
                 tp = ps_t.tile([P, 2, 2, NA], F32, name="tp", tag="tp")
                 for a in range(2):
-                    jj = off + 2 * h + a
+                    jj = 2 * h + a
                     for u in range(2):
                         nc.tensor.transpose(tp[:, a, u, :], d32[:, jj * 256 + u * P:jj * 256 + (u + 1) * P],
                                             ident[:])
-                nc.scalar.copy(out=g32[:, h], in_=tp[:].rearrange("p a u i -> p a i u"))
-            d_codes = work.tile([P, QJ * NA], U32, name="d_codes", tag="d_codes", align_bytes=64)
-            d_scales = work.tile([P, QJ * NA], U8, name="d_scales", tag="d_scales", align_bytes=64)
-            nc.vector.quantize_mx(out=d_codes[:].bitcast(FP8X4), scales=d_scales[:], in_=d_grp[:])
+                tps.append(tp)
+            st[("t", q)] = tps
+
+        def evacuate(q):
+            d_grp = work.tile([P, W * 4], BF16, name="d_grp", tag="d_grp", align_bytes=64)
+            g32 = d_grp[:].bitcast(F32).rearrange("p (h a i u) -> p h a i u", h=2, a=2, u=2)
+            for h in range(2):
+                nc.scalar.copy(out=g32[:, h], in_=st[("t", q)][h][:].rearrange("p a u i -> p a i u"))
+            st[("dg", q)] = d_grp
+
+        def quantise_d(q):
+            d_codes = work.tile([P, W], U32, name="d_codes", tag="d_codes", align_bytes=64)
+            d_scales = work.tile([P, W], U8, name="d_scales", tag="d_scales", align_bytes=64)
+            nc.vector.quantize_mx(out=d_codes[:].bitcast(FP8X4), scales=d_scales[:], in_=st[("dg", q)][:])
             st[("d", q)] = (d_codes, d_scales)
 
-        def stage_b(q):
+        def mx1(q, c):
             d_codes, d_scales = st[("d", q)]
-            planes = work.tile([P, 4, QJ * NA], BF16, name="planes", tag="planes")
-            j0 = q * QJ
-            for c in range(4):
-                p1 = ps_1.tile([P, QJ * NA], F32, name="p1", tag="p1")
-                nc.tensor.matmul_mx(out=p1[:], lhsT=w_codes[:, c * P:(c + 1) * P].bitcast(FP8X4),
-                                    lhsT_scale=w_scales[:, c * P:(c + 1) * P],
-                                    rhs=d_codes[:].bitcast(FP8X4), rhs_scale=d_scales[:],
-                                    start=True, stop=True)
-                if c in SC_CHUNKS[q % 2]:
-                    for a in range(QJ):
-                        nc.scalar.activation(out=planes[:, c, a * NA:(a + 1) * NA], in_=p1[:, a * NA:(a + 1) * NA],
-                                             func=ACT.Identity, scale=gate[:, c, j0 + a:j0 + a + 1],
-                                             bias=gbias[:, c, j0 + a:j0 + a + 1])
-                else:
-                    nc.vector.scalar_tensor_tensor(
-                        out=planes[:, c, :].rearrange("p (a i) -> p a i", a=QJ),
-                        in0=p1[:].rearrange("p (a i) -> p a i", a=QJ),
-                        scalar=bdf[:, c:c + 1],
-                        in1=gate[:, c, j0:j0 + QJ].unsqueeze(2).to_broadcast([P, QJ, NA]),
-                        op0=ALU.add, op1=ALU.mult)
-            st[("p", q)] = planes
+            p1 = ps_1.tile([P, W], F32, name="p1", tag="p1")
+            nc.tensor.matmul_mx(out=p1[:], lhsT=w_codes[:, c * P:(c + 1) * P].bitcast(FP8X4),
+                                lhsT_scale=w_scales[:, c * P:(c + 1) * P],
+                                rhs=d_codes[:].bitcast(FP8X4), rhs_scale=d_scales[:],
+                                start=True, stop=True)
+            st[("p1", q, c)] = p1
 
-        def stage_c(q):
-            planes = st[("p", q)]
-            g_grp = work.tile([P, QJ * NA, 4], BF16, name="g_grp", tag="g_grp", align_bytes=64)
+        def gate_scalar(q, c):
+            p1 = st[("p1", q, c)]
+            planes = st[("pl", q)]
+            j0 = q * QJ
+            for a in range(QJ):
+                nc.scalar.activation(out=planes[:, c, a * NA:(a + 1) * NA], in_=p1[:, a * NA:(a + 1) * NA],
+                                     func=ACT.Identity, scale=gate[:, c, j0 + a:j0 + a + 1],
+                                     bias=gbias[:, c, j0 + a:j0 + a + 1])
+
+        def gate_vector(q, c):
+            p1 = st[("p1", q, c)]
+            planes = st[("pl", q)]
+            j0 = q * QJ
+            nc.vector.scalar_tensor_tensor(
+                out=planes[:, c, :].rearrange("p (a i) -> p a i", a=QJ),
+                in0=p1[:].rearrange("p (a i) -> p a i", a=QJ),
+                scalar=bdf[:, c:c + 1],
+                in1=gate[:, c, j0:j0 + QJ].unsqueeze(2).to_broadcast([P, QJ, NA]),
+                op0=ALU.add, op1=ALU.mult)
+
+        def regroup(q):
+            g_grp = work.tile([P, W, 4], BF16, name="g_grp", tag="g_grp", align_bytes=64)
             nc.vector.tensor_copy(out=g_grp[:].rearrange("p (x y) t -> p x t y", y=4),
-                                  in_=planes[:].rearrange("p t (x y) -> p x t y", y=4))
-            g_codes = work.tile([P, QJ * NA], U32, name="g_codes", tag="g_codes", align_bytes=64)
-            g_scales = work.tile([P, QJ * NA], U8, name="g_scales", tag="g_scales", align_bytes=64)
+                                  in_=st[("pl", q)][:].rearrange("p t (x y) -> p x t y", y=4))
+            st[("gg", q)] = g_grp
+
+        def quantise_g(q):
+            g_codes = work.tile([P, W], U32, name="g_codes", tag="g_codes", align_bytes=64)
+            g_scales = work.tile([P, W], U8, name="g_scales", tag="g_scales", align_bytes=64)
             nc.vector.quantize_mx(out=g_codes[:].bitcast(FP8X4), scales=g_scales[:],
-                                  in_=g_grp[:].rearrange("p w t -> p (w t)"))
+                                  in_=st[("gg", q)][:].rearrange("p w t -> p (w t)"))
             st[("g", q)] = (g_codes, g_scales)
 
-        def stage_d(q):
+        def mx2(q):
             g_codes, g_scales = st[("g", q)]
-            j0 = q * QJ
             p2 = ps_2.tile([P, QJ, NF], F32, name="p2", tag="p2")
-            th = work.tile([P, QJ, NF], F32, name="th", tag="th")
             for a in range(QJ):
                 nc.tensor.matmul_mx(out=p2[:, a, :], lhsT=g_codes[:, a * NA:(a + 1) * NA].bitcast(FP8X4),
                                     lhsT_scale=g_scales[:, a * NA:(a + 1) * NA],
                                     rhs=f_codes[:].bitcast(FP8X4), rhs_scale=f_scales[:],
                                     start=True, stop=True)
+            st[("p2", q)] = p2
+
+        def tanh(q):
+            p2 = st[("p2", q)]
+            j0 = q * QJ
+            th = work.tile([P, QJ, NF], F32, name="th", tag="th")
             for a in range(QJ):
                 nc.scalar.activation(out=th[:, a, :], in_=p2[:, a, :], func=ACT.Tanh,
                                      scale=mask[:, j0 + a:j0 + a + 1])
+            st[("th", q)] = th
+
+        def add_up(q):
+            th = st[("th", q)]
             for a in range(QJ):
                 nc.tensor.matmul(accT[:], lhsT=th[:, a, :], rhs=ident[:], start=False,
                                  stop=(q == NQ - 1 and a == QJ - 1), is_transpose=True)
 
-        for s in range(NQ + 3):
-            if s < NQ:
-                stage_a(s)
-            if 0 <= s - 1 < NQ:
-                stage_b(s - 1)
-            if 0 <= s - 2 < NQ:
-                stage_c(s - 2)
-            if 0 <= s - 3 < NQ:
-                stage_d(s - 3)
+        def live(q):
+            return 0 <= q < NQ
+
+        for s in range(NQ + 6):
+            if live(s - 5):
+                add_up(s - 5)
+            if live(s):
+                transposes(s)
+            if live(s + LOADS_AHEAD):
+                load(s + LOADS_AHEAD)
+            if live(s - 4):
+                tanh(s - 4)
+            if live(s):
+                evacuate(s)
+            if s == 0:
+                for c in range(4):
+                    nc.scalar.activation(out=gbias[:, c, :], in_=gate[:, c, :], func=ACT.Copy,
+                                         scale=bdf[:, c:c + 1])
+            if live(s - 2):
+                regroup(s - 2)
+            vec = []
+            if live(s - 1):
+                q = s - 1
+                planes = work.tile([P, 4, W], BF16, name="planes", tag="planes")
+                st[("pl", q)] = planes
+                for c, eng in PASSES[q % 3]:
+                    mx1(q, c)
+                for c, eng in PASSES[q % 3]:
+                    if eng == "s":
+                        gate_scalar(q, c)
+                    else:
+                        vec.append(c)
+            if live(s - 3):
+                mx2(s - 3)
+            if vec:
+                gate_vector(s - 1, vec[0])
+            if live(s - 2):
+                quantise_g(s - 2)
+            for c in vec[1:]:
+                gate_vector(s - 1, c)
+            if live(s):
+                quantise_d(s)
+            if s == 0:
+                nc.vector.quantize_mx(out=f_codes[:].bitcast(FP8X4), scales=f_scales[:],
+                                      in_=f_grp[:].rearrange("p f t -> p (f t)"))
 
         sumT = const.tile([P, NA], F32, name="sumT")
         nc.vector.tensor_copy(out=sumT[:], in_=accT[:])

@@ -22,11 +22,7 @@ W = QJ * NA
 LOADS_AHEAD = 6
 FLOPS = 2 * NA * NA * ND * NH + 2 * NA * NA * NH * NF + 2 * NA * NF * NH
 
-PASSES = (
-    ((3, "v"), (0, "s"), (1, "s"), (2, "v")),
-    ((3, "v"), (0, "s"), (1, "s"), (2, "v")),
-    ((3, "v"), (0, "s"), (1, "s"), (2, "s")),
-)
+CHUNKS = (3, 0, 1, 2)
 
 
 def tile_dtnnstep_pa_t_kernel(tc, atom_features, distance_matrix, distance_matrix_mask,
@@ -42,8 +38,8 @@ def tile_dtnnstep_pa_t_kernel(tc, atom_features, distance_matrix, distance_matri
         dpool = ctx.enter_context(tc.tile_pool(name="dpool", bufs=LOADS_AHEAD))
         work = ctx.enter_context(tc.tile_pool(name="work", bufs=3))
         ps_t = ctx.enter_context(tc.psum_pool(name="ps_t", bufs=2))
-        ps_1 = ctx.enter_context(tc.psum_pool(name="ps_1", bufs=4))
-        ps_2 = ctx.enter_context(tc.psum_pool(name="ps_2", bufs=1))
+        ps_1 = ctx.enter_context(tc.psum_pool(name="ps_1", bufs=2))
+        ps_2 = ctx.enter_context(tc.psum_pool(name="ps_2", bufs=2))
         ps_a = ctx.enter_context(tc.psum_pool(name="ps_a", bufs=1))
         ctx.enter_context(tc.manual_schedule())
 
@@ -93,7 +89,7 @@ def tile_dtnnstep_pa_t_kernel(tc, atom_features, distance_matrix, distance_matri
         nc.tensor.transpose(aT_ps[:], a32[:], ident[:])
         aT = const.tile([P, NA], BF16, name="aT")
         nc.scalar.copy(out=aT[:], in_=aT_ps[:])
-        at_ps = ps_1.tile([P, 4, NA], F32, name="at_ps", tag="p1")
+        at_ps = ps_2.tile([P, 4, NA], F32, name="at_ps", tag="p2")
         for c in range(4):
             nc.tensor.matmul(at_ps[:, c, :], lhsT=wcf[:, c, :], rhs=aT[:], start=True, stop=True)
         accT = ps_a.tile([P, NA], F32, name="accT")
@@ -121,31 +117,32 @@ def tile_dtnnstep_pa_t_kernel(tc, atom_features, distance_matrix, distance_matri
 
         st = {}
 
-        def transposes(q):
+        def transposes(q, h):
             d32 = dtiles[q][:].bitcast(F32)
-            tps = []
-            for h in range(2):
-                tp = ps_t.tile([P, 2, 2, NA], F32, name="tp", tag="tp")
-                for a in range(2):
-                    jj = 2 * h + a
-                    for u in range(2):
-                        nc.tensor.transpose(tp[:, a, u, :], d32[:, jj * 256 + u * P:jj * 256 + (u + 1) * P],
-                                            ident[:])
-                tps.append(tp)
-            st[("t", q)] = tps
+            tp = ps_t.tile([P, 2, 2, NA], F32, name="tp", tag="tp")
+            for a in range(2):
+                jj = 2 * h + a
+                for u in range(2):
+                    nc.tensor.transpose(tp[:, a, u, :], d32[:, jj * 256 + u * P:jj * 256 + (u + 1) * P], ident[:])
+            st[("t", q, h)] = tp
 
-        def evacuate(q):
-            d_grp = work.tile([P, W * 4], BF16, name="d_grp", tag="d_grp", align_bytes=64)
-            g32 = d_grp[:].bitcast(F32).rearrange("p (h a i u) -> p h a i u", h=2, a=2, u=2)
-            for h in range(2):
-                nc.scalar.copy(out=g32[:, h], in_=st[("t", q)][h][:].rearrange("p a u i -> p a i u"))
-            st[("dg", q)] = d_grp
+        def evacuate(q, h):
+            if h == 0:
+                d_grp = work.tile([P, W * 4], BF16, name="d_grp", tag="d_grp", align_bytes=64)
+                st[("dg", q)] = d_grp
+            g32 = st[("dg", q)][:].bitcast(F32).rearrange("p (h a i u) -> p h a i u", h=2, a=2, u=2)
+            nc.scalar.copy(out=g32[:, h], in_=st[("t", q, h)][:].rearrange("p a u i -> p a i u"))
 
-        def quantise_d(q):
-            d_codes = work.tile([P, W], U32, name="d_codes", tag="d_codes", align_bytes=64)
-            d_scales = work.tile([P, W], U8, name="d_scales", tag="d_scales", align_bytes=64)
-            nc.vector.quantize_mx(out=d_codes[:].bitcast(FP8X4), scales=d_scales[:], in_=st[("dg", q)][:])
-            st[("d", q)] = (d_codes, d_scales)
+        def quantise_d(q, h):
+            if h == 0:
+                d_codes = work.tile([P, W], U32, name="d_codes", tag="d_codes", align_bytes=64)
+                d_scales = work.tile([P, W], U8, name="d_scales", tag="d_scales", align_bytes=64)
+                st[("d", q)] = (d_codes, d_scales)
+            d_codes, d_scales = st[("d", q)]
+            hw = W // 2
+            nc.vector.quantize_mx(out=d_codes[:, h * hw:(h + 1) * hw].bitcast(FP8X4),
+                                  scales=d_scales[:, h * hw:(h + 1) * hw],
+                                  in_=st[("dg", q)][:, h * hw * 4:(h + 1) * hw * 4])
 
         def mx1(q, c):
             d_codes, d_scales = st[("d", q)]
@@ -189,15 +186,17 @@ def tile_dtnnstep_pa_t_kernel(tc, atom_features, distance_matrix, distance_matri
                                   in_=st[("gg", q)][:].rearrange("p w t -> p (w t)"))
             st[("g", q)] = (g_codes, g_scales)
 
-        def mx2(q):
+        def mx2(q, h):
             g_codes, g_scales = st[("g", q)]
-            p2 = ps_2.tile([P, QJ, NF], F32, name="p2", tag="p2")
-            for a in range(QJ):
+            if h == 0:
+                p2 = ps_2.tile([P, QJ, NF], F32, name="p2", tag="p2")
+                st[("p2", q)] = p2
+            p2 = st[("p2", q)]
+            for a in (2 * h, 2 * h + 1):
                 nc.tensor.matmul_mx(out=p2[:, a, :], lhsT=g_codes[:, a * NA:(a + 1) * NA].bitcast(FP8X4),
                                     lhsT_scale=g_scales[:, a * NA:(a + 1) * NA],
                                     rhs=f_codes[:].bitcast(FP8X4), rhs_scale=f_scales[:],
                                     start=True, stop=True)
-            st[("p2", q)] = p2
 
         def tanh(q):
             p2 = st[("p2", q)]
@@ -208,54 +207,62 @@ def tile_dtnnstep_pa_t_kernel(tc, atom_features, distance_matrix, distance_matri
                                      scale=mask[:, j0 + a:j0 + a + 1])
             st[("th", q)] = th
 
-        def add_up(q):
+        def add_up(q, h):
             th = st[("th", q)]
-            for a in range(QJ):
+            for a in (2 * h, 2 * h + 1):
                 nc.tensor.matmul(accT[:], lhsT=th[:, a, :], rhs=ident[:], start=False,
                                  stop=(q == NQ - 1 and a == QJ - 1), is_transpose=True)
 
         def live(q):
             return 0 <= q < NQ
 
+        transposes(0, 0)
         for s in range(NQ + 6):
-            if live(s - 5):
-                add_up(s - 5)
-            if live(s):
-                transposes(s)
-            if live(s + LOADS_AHEAD):
-                load(s + LOADS_AHEAD)
+            if live(s - 1):
+                planes = work.tile([P, 4, W], BF16, name="planes", tag="planes")
+                st[("pl", s - 1)] = planes
+                mx1(s - 1, CHUNKS[0])
+                mx1(s - 1, CHUNKS[1])
+            if live(s - 3):
+                mx2(s - 3, 0)
             if live(s - 4):
                 tanh(s - 4)
+            if live(s - 5):
+                add_up(s - 5, 0)
             if live(s):
-                evacuate(s)
+                transposes(s, 1)
+            if live(s + LOADS_AHEAD):
+                load(s + LOADS_AHEAD)
+            if live(s):
+                evacuate(s, 0)
+            if live(s - 2):
+                regroup(s - 2)
+            if live(s - 1):
+                gate_vector(s - 1, CHUNKS[0])
+                gate_scalar(s - 1, CHUNKS[1])
+            if live(s - 1):
+                mx1(s - 1, CHUNKS[2])
+                mx1(s - 1, CHUNKS[3])
+            if live(s - 3):
+                mx2(s - 3, 1)
+            if live(s - 2):
+                quantise_g(s - 2)
+            if live(s):
+                quantise_d(s, 0)
+                evacuate(s, 1)
             if s == 0:
                 for c in range(4):
                     nc.scalar.activation(out=gbias[:, c, :], in_=gate[:, c, :], func=ACT.Copy,
                                          scale=bdf[:, c:c + 1])
-            if live(s - 2):
-                regroup(s - 2)
-            vec = []
             if live(s - 1):
-                q = s - 1
-                planes = work.tile([P, 4, W], BF16, name="planes", tag="planes")
-                st[("pl", q)] = planes
-                for c, eng in PASSES[q % 3]:
-                    mx1(q, c)
-                for c, eng in PASSES[q % 3]:
-                    if eng == "s":
-                        gate_scalar(q, c)
-                    else:
-                        vec.append(c)
-            if live(s - 3):
-                mx2(s - 3)
-            if vec:
-                gate_vector(s - 1, vec[0])
-            if live(s - 2):
-                quantise_g(s - 2)
-            for c in vec[1:]:
-                gate_vector(s - 1, c)
+                gate_scalar(s - 1, CHUNKS[2])
+                gate_vector(s - 1, CHUNKS[3])
+            if live(s - 5):
+                add_up(s - 5, 1)
+            if live(s + 1):
+                transposes(s + 1, 0)
             if live(s):
-                quantise_d(s)
+                quantise_d(s, 1)
             if s == 0:
                 nc.vector.quantize_mx(out=f_codes[:].bitcast(FP8X4), scales=f_scales[:],
                                       in_=f_grp[:].rearrange("p f t -> p (f t)"))

@@ -22,7 +22,11 @@ W = QJ * NA
 LOADS_AHEAD = 6
 FLOPS = 2 * NA * NA * ND * NH + 2 * NA * NA * NH * NF + 2 * NA * NF * NH
 
-CHUNKS = (3, 0, 1, 2)
+PASSES = (
+    ((3, "v"), (0, "s"), (1, "s"), (2, "v")),
+    ((3, "v"), (0, "s"), (1, "s"), (2, "v")),
+    ((3, "v"), (0, "s"), (1, "s"), (2, "s")),
+)
 
 
 def tile_dtnnstep_pa_t_kernel(tc, atom_features, distance_matrix, distance_matrix_mask,
@@ -36,10 +40,10 @@ def tile_dtnnstep_pa_t_kernel(tc, atom_features, distance_matrix, distance_matri
     with ExitStack() as ctx:
         const = ctx.enter_context(tc.tile_pool(name="const", bufs=1))
         dpool = ctx.enter_context(tc.tile_pool(name="dpool", bufs=LOADS_AHEAD))
-        work = ctx.enter_context(tc.tile_pool(name="work", bufs=3))
+        work = ctx.enter_context(tc.tile_pool(name="work", bufs=4))
         ps_t = ctx.enter_context(tc.psum_pool(name="ps_t", bufs=2))
-        ps_1 = ctx.enter_context(tc.psum_pool(name="ps_1", bufs=2))
-        ps_2 = ctx.enter_context(tc.psum_pool(name="ps_2", bufs=2))
+        ps_1 = ctx.enter_context(tc.psum_pool(name="ps_1", bufs=4))
+        ps_2 = ctx.enter_context(tc.psum_pool(name="ps_2", bufs=1))
         ps_a = ctx.enter_context(tc.psum_pool(name="ps_a", bufs=1))
         ctx.enter_context(tc.manual_schedule())
 
@@ -117,32 +121,31 @@ def tile_dtnnstep_pa_t_kernel(tc, atom_features, distance_matrix, distance_matri
 
         st = {}
 
-        def transposes(q, h):
+        def transposes(q):
             d32 = dtiles[q][:].bitcast(F32)
-            tp = ps_t.tile([P, 2, 2, NA], F32, name="tp", tag="tp")
-            for a in range(2):
-                jj = 2 * h + a
-                for u in range(2):
-                    nc.tensor.transpose(tp[:, a, u, :], d32[:, jj * 256 + u * P:jj * 256 + (u + 1) * P], ident[:])
-            st[("t", q, h)] = tp
+            tps = []
+            for h in range(2):
+                tp = ps_t.tile([P, 2, 2, NA], F32, name="tp", tag="tp")
+                for a in range(2):
+                    jj = 2 * h + a
+                    for u in range(2):
+                        nc.tensor.transpose(tp[:, a, u, :], d32[:, jj * 256 + u * P:jj * 256 + (u + 1) * P],
+                                            ident[:])
+                tps.append(tp)
+            st[("t", q)] = tps
 
-        def evacuate(q, h):
-            if h == 0:
-                d_grp = work.tile([P, W * 4], BF16, name="d_grp", tag="d_grp", align_bytes=64)
-                st[("dg", q)] = d_grp
-            g32 = st[("dg", q)][:].bitcast(F32).rearrange("p (h a i u) -> p h a i u", h=2, a=2, u=2)
-            nc.scalar.copy(out=g32[:, h], in_=st[("t", q, h)][:].rearrange("p a u i -> p a i u"))
+        def evacuate(q):
+            d_grp = work.tile([P, W * 4], BF16, name="d_grp", tag="d_grp", align_bytes=64)
+            g32 = d_grp[:].bitcast(F32).rearrange("p (h a i u) -> p h a i u", h=2, a=2, u=2)
+            for h in range(2):
+                nc.scalar.copy(out=g32[:, h], in_=st[("t", q)][h][:].rearrange("p a u i -> p a i u"))
+            st[("dg", q)] = d_grp
 
-        def quantise_d(q, h):
-            if h == 0:
-                d_codes = work.tile([P, W], U32, name="d_codes", tag="d_codes", align_bytes=64)
-                d_scales = work.tile([P, W], U8, name="d_scales", tag="d_scales", align_bytes=64)
-                st[("d", q)] = (d_codes, d_scales)
-            d_codes, d_scales = st[("d", q)]
-            hw = W // 2
-            nc.vector.quantize_mx(out=d_codes[:, h * hw:(h + 1) * hw].bitcast(FP8X4),
-                                  scales=d_scales[:, h * hw:(h + 1) * hw],
-                                  in_=st[("dg", q)][:, h * hw * 4:(h + 1) * hw * 4])
+        def quantise_d(q):
+            d_codes = work.tile([P, W], U32, name="d_codes", tag="d_codes", align_bytes=64)
+            d_scales = work.tile([P, W], U8, name="d_scales", tag="d_scales", align_bytes=64)
+            nc.vector.quantize_mx(out=d_codes[:].bitcast(FP8X4), scales=d_scales[:], in_=st[("dg", q)][:])
+            st[("d", q)] = (d_codes, d_scales)
 
         def mx1(q, c):
             d_codes, d_scales = st[("d", q)]
@@ -186,17 +189,15 @@ def tile_dtnnstep_pa_t_kernel(tc, atom_features, distance_matrix, distance_matri
                                   in_=st[("gg", q)][:].rearrange("p w t -> p (w t)"))
             st[("g", q)] = (g_codes, g_scales)
 
-        def mx2(q, h):
+        def mx2(q):
             g_codes, g_scales = st[("g", q)]
-            if h == 0:
-                p2 = ps_2.tile([P, QJ, NF], F32, name="p2", tag="p2")
-                st[("p2", q)] = p2
-            p2 = st[("p2", q)]
-            for a in (2 * h, 2 * h + 1):
+            p2 = ps_2.tile([P, QJ, NF], F32, name="p2", tag="p2")
+            for a in range(QJ):
                 nc.tensor.matmul_mx(out=p2[:, a, :], lhsT=g_codes[:, a * NA:(a + 1) * NA].bitcast(FP8X4),
                                     lhsT_scale=g_scales[:, a * NA:(a + 1) * NA],
                                     rhs=f_codes[:].bitcast(FP8X4), rhs_scale=f_scales[:],
                                     start=True, stop=True)
+            st[("p2", q)] = p2
 
         def tanh(q):
             p2 = st[("p2", q)]
@@ -207,62 +208,56 @@ def tile_dtnnstep_pa_t_kernel(tc, atom_features, distance_matrix, distance_matri
                                      scale=mask[:, j0 + a:j0 + a + 1])
             st[("th", q)] = th
 
-        def add_up(q, h):
+        def add_up(q):
             th = st[("th", q)]
-            for a in (2 * h, 2 * h + 1):
+            for a in range(QJ):
                 nc.tensor.matmul(accT[:], lhsT=th[:, a, :], rhs=ident[:], start=False,
                                  stop=(q == NQ - 1 and a == QJ - 1), is_transpose=True)
 
         def live(q):
             return 0 <= q < NQ
 
-        transposes(0, 0)
-        for s in range(NQ + 6):
-            if live(s - 1):
+        for s in range(NQ + 7):
+            q1 = s - 2
+            passes = PASSES[q1 % 3] if live(q1) else ()
+            if live(q1):
                 planes = work.tile([P, 4, W], BF16, name="planes", tag="planes")
-                st[("pl", s - 1)] = planes
-                mx1(s - 1, CHUNKS[0])
-                mx1(s - 1, CHUNKS[1])
-            if live(s - 3):
-                mx2(s - 3, 0)
-            if live(s - 4):
-                tanh(s - 4)
-            if live(s - 5):
-                add_up(s - 5, 0)
+                st[("pl", q1)] = planes
+                for c, eng in passes[0:2]:
+                    mx1(q1, c)
+            if live(s - 6):
+                add_up(s - 6)
             if live(s):
-                transposes(s, 1)
+                transposes(s)
             if live(s + LOADS_AHEAD):
                 load(s + LOADS_AHEAD)
+            if live(s - 5):
+                tanh(s - 5)
             if live(s):
-                evacuate(s, 0)
-            if live(s - 2):
-                regroup(s - 2)
-            if live(s - 1):
-                gate_vector(s - 1, CHUNKS[0])
-                gate_scalar(s - 1, CHUNKS[1])
-            if live(s - 1):
-                mx1(s - 1, CHUNKS[2])
-                mx1(s - 1, CHUNKS[3])
-            if live(s - 3):
-                mx2(s - 3, 1)
-            if live(s - 2):
-                quantise_g(s - 2)
-            if live(s):
-                quantise_d(s, 0)
-                evacuate(s, 1)
+                evacuate(s)
             if s == 0:
                 for c in range(4):
                     nc.scalar.activation(out=gbias[:, c, :], in_=gate[:, c, :], func=ACT.Copy,
                                          scale=bdf[:, c:c + 1])
-            if live(s - 1):
-                gate_scalar(s - 1, CHUNKS[2])
-                gate_vector(s - 1, CHUNKS[3])
-            if live(s - 5):
-                add_up(s - 5, 1)
-            if live(s + 1):
-                transposes(s + 1, 0)
+            if live(q1):
+                for c, eng in passes[2:4]:
+                    mx1(q1, c)
+            if live(s - 4):
+                mx2(s - 4)
+            for c, eng in passes:
+                if eng == "s":
+                    gate_scalar(q1, c)
+            vec = [c for c, eng in passes if eng == "v"]
+            if live(s - 3):
+                regroup(s - 3)
+            if vec:
+                gate_vector(q1, vec[0])
+            if live(s - 3):
+                quantise_g(s - 3)
+            for c in vec[1:]:
+                gate_vector(q1, c)
             if live(s):
-                quantise_d(s, 1)
+                quantise_d(s)
             if s == 0:
                 nc.vector.quantize_mx(out=f_codes[:].bitcast(FP8X4), scales=f_scales[:],
                                       in_=f_grp[:].rearrange("p f t -> p (f t)"))

@@ -20,12 +20,13 @@ QJ = 4
 NQ = NA // QJ
 W = QJ * NA
 LOADS_AHEAD = 6
+W_VEC = 3 * W // 4
 FLOPS = 2 * NA * NA * ND * NH + 2 * NA * NA * NH * NF + 2 * NA * NF * NH
 
 PASSES = (
     ((3, "v"), (0, "s"), (1, "s"), (2, "v")),
     ((3, "v"), (0, "s"), (1, "s"), (2, "v")),
-    ((3, "v"), (0, "s"), (1, "s"), (2, "s")),
+    ((3, "v"), (0, "s"), (1, "s"), (2, "v")),
 )
 
 
@@ -41,6 +42,7 @@ def tile_dtnnstep_pa_t_kernel(tc, atom_features, distance_matrix, distance_matri
         const = ctx.enter_context(tc.tile_pool(name="const", bufs=1))
         dpool = ctx.enter_context(tc.tile_pool(name="dpool", bufs=LOADS_AHEAD))
         work = ctx.enter_context(tc.tile_pool(name="work", bufs=4))
+        gpool = ctx.enter_context(tc.tile_pool(name="gpool", bufs=1))
         ps_t = ctx.enter_context(tc.psum_pool(name="ps_t", bufs=2))
         ps_1 = ctx.enter_context(tc.psum_pool(name="ps_1", bufs=4))
         ps_2 = ctx.enter_context(tc.psum_pool(name="ps_2", bufs=1))
@@ -176,11 +178,16 @@ def tile_dtnnstep_pa_t_kernel(tc, atom_features, distance_matrix, distance_matri
                 in1=gate[:, c, j0:j0 + QJ].unsqueeze(2).to_broadcast([P, QJ, NA]),
                 op0=ALU.add, op1=ALU.mult)
 
-        def regroup(q):
-            g_grp = work.tile([P, W, 4], BF16, name="g_grp", tag="g_grp", align_bytes=64)
-            nc.vector.tensor_copy(out=g_grp[:].rearrange("p (x y) t -> p x t y", y=4),
-                                  in_=st[("pl", q)][:].rearrange("p t (x y) -> p x t y", y=4))
+        def regroup_gpsimd(q):
+            g_grp = gpool.tile([P, W, 4], BF16, name="g_grp", tag="g_grp", align_bytes=64)
+            nc.gpsimd.tensor_scalar(out=g_grp[:, W_VEC:, :], in0=st[("pl", q)][:, :, W_VEC:].rearrange("p t w -> p w t"),
+                                    scalar1=1.0, scalar2=0.0, op0=ALU.mult, op1=ALU.add)
             st[("gg", q)] = g_grp
+
+        def regroup(q):
+            g_grp = st[("gg", q)]
+            nc.vector.tensor_copy(out=g_grp[:, :W_VEC, :].rearrange("p (x y) t -> p x t y", y=4),
+                                  in_=st[("pl", q)][:, :, :W_VEC].rearrange("p t (x y) -> p x t y", y=4))
 
         def quantise_g(q):
             g_codes = work.tile([P, W], U32, name="g_codes", tag="g_codes", align_bytes=64)
@@ -220,6 +227,10 @@ def tile_dtnnstep_pa_t_kernel(tc, atom_features, distance_matrix, distance_matri
         for s in range(NQ + 7):
             q1 = s - 2
             passes = PASSES[q1 % 3] if live(q1) else ()
+            if live(s - 4):
+                quantise_g(s - 4)
+            if live(s - 3):
+                regroup_gpsimd(s - 3)
             if live(q1):
                 planes = work.tile([P, 4, W], BF16, name="planes", tag="planes")
                 st[("pl", q1)] = planes
@@ -248,14 +259,10 @@ def tile_dtnnstep_pa_t_kernel(tc, atom_features, distance_matrix, distance_matri
                 if eng == "s":
                     gate_scalar(q1, c)
             vec = [c for c, eng in passes if eng == "v"]
+            for c in vec:
+                gate_vector(q1, c)
             if live(s - 3):
                 regroup(s - 3)
-            if vec:
-                gate_vector(q1, vec[0])
-            if live(s - 3):
-                quantise_g(s - 3)
-            for c in vec[1:]:
-                gate_vector(q1, c)
             if live(s):
                 quantise_d(s)
             if s == 0:

@@ -49,77 +49,45 @@ def tile_dtnnstep_pa_t_kernel(tc, atom_features, distance_matrix, distance_matri
         ps_a = ctx.enter_context(tc.psum_pool(name="ps_a", bufs=1))
         ctx.enter_context(tc.manual_schedule())
 
-        w_raw = const.tile([P, 4, NH], BF16, name="w_raw")
-        for u in range(2):
-            nc.sync.dma_start(out=w_raw[:, 2 * u:2 * u + 2, :],
-                              in_=W_df[256 * u:256 * u + 256, :].rearrange("(q e) h -> q e h", e=2))
         dtiles = {}
 
-        def load(q):
+        def load(q, pieces=1):
             dt_ = dpool.tile([P, QJ * ND], BF16, name="dt_", tag="dt_")
-            nc.sync.dma_start(out=dt_[:], in_=d_dram[:, q * QJ * ND:(q + 1) * QJ * ND])
+            n = QJ * ND // pieces
+            for u in range(pieces):
+                nc.sync.dma_start(out=dt_[:, u * n:(u + 1) * n],
+                                  in_=d_dram[:, q * QJ * ND + u * n:q * QJ * ND + (u + 1) * n])
             dtiles[q] = dt_
 
-        for q in range(LOADS_AHEAD):
-            load(q)
         a_bf = const.tile([P, NF], BF16, name="a_bf")
         nc.scalar.dma_start(out=a_bf[:], in_=a_dram)
         wcf_raw = const.tile([P, NH], BF16, name="wcf_raw")
         nc.scalar.dma_start(out=wcf_raw[:], in_=W_cf)
-        bcf_bf = const.tile([P, 4], BF16, name="bcf_bf")
-        nc.scalar.dma_start(out=bcf_bf[:], in_=b_cf.rearrange("(m c) -> m c", c=4))
-        bdf_bf = const.tile([P, 4], BF16, name="bdf_bf")
-        nc.scalar.dma_start(out=bdf_bf[:], in_=b_df.rearrange("(m c) -> m c", c=4))
+        load(0, pieces=2)
+        w_raw = const.tile([P, 4, NH], BF16, name="w_raw")
+        for u in range(2):
+            nc.sync.dma_start(out=w_raw[:, 2 * u:2 * u + 2, :],
+                              in_=W_df[256 * u:256 * u + 256, :].rearrange("(q e) h -> q e h", e=2))
+        bcf = const.tile([P, 4], BF16, name="bcf")
+        nc.scalar.dma_start(out=bcf[:], in_=b_cf.rearrange("(m c) -> m c", c=4))
+        bdf = const.tile([P, 4], BF16, name="bdf")
+        nc.scalar.dma_start(out=bdf[:], in_=b_df.rearrange("(m c) -> m c", c=4))
+        load(1)
+        load(2)
         f_raw = const.tile([P, 4, NF], BF16, name="f_raw")
-        nc.scalar.dma_start(out=f_raw[:], in_=W_fc.rearrange("(p t) f -> p t f", t=4))
+        nc.sync.dma_start(out=f_raw[:], in_=W_fc.rearrange("(p t) f -> p t f", t=4))
         m_bf = const.tile([P, NA], BF16, name="m_bf")
-        nc.scalar.dma_start(out=m_bf[:], in_=m_dram)
+        nc.sync.dma_start(out=m_bf[:], in_=m_dram)
+        for q in range(3, LOADS_AHEAD):
+            load(q)
 
         ident = const.tile([P, P], F32, name="ident")
         make_identity(nc, ident[:])
-        a32 = const.tile([P, NF], F32, name="a32")
-        nc.gpsimd.tensor_copy(out=a32[:], in_=a_bf[:])
-        bcf = const.tile([P, 4], F32, name="bcf")
-        nc.gpsimd.tensor_copy(out=bcf[:], in_=bcf_bf[:])
-        bdf = const.tile([P, 4], F32, name="bdf")
-        nc.gpsimd.tensor_copy(out=bdf[:], in_=bdf_bf[:])
         f_grp = const.tile([P, NF, 4], BF16, name="f_grp", align_bytes=64)
         nc.gpsimd.tensor_scalar(out=f_grp[:], in0=f_raw[:].rearrange("p t f -> p f t"), scalar1=1.0, scalar2=0.0,
                                 op0=ALU.mult, op1=ALU.add)
         mask = const.tile([P, NA], F32, name="mask")
         nc.gpsimd.tensor_scalar(out=mask[:], in0=m_bf[:], scalar1=1.0, scalar2=0.0, op0=ALU.mult, op1=ALU.add)
-
-        wcf = const.tile([P, 4, P], BF16, name="wcf")
-        nc.scalar.copy(out=wcf[:], in_=wcf_raw[:].rearrange("f (m c) -> f c m", c=4))
-        aT_ps = ps_t.tile([P, P], F32, name="aT_ps", tag="tp")
-        nc.tensor.transpose(aT_ps[:], a32[:], ident[:])
-        aT = const.tile([P, NA], BF16, name="aT")
-        nc.scalar.copy(out=aT[:], in_=aT_ps[:])
-        at_ps = ps_2.tile([P, 4, NA], F32, name="at_ps", tag="p2")
-        for c in range(4):
-            nc.tensor.matmul(at_ps[:, c, :], lhsT=wcf[:, c, :], rhs=aT[:], start=True, stop=True)
-        accT = ps_a.tile([P, NA], F32, name="accT")
-        nc.tensor.matmul(accT[:], lhsT=a32[:], rhs=ident[:], start=True, stop=False, is_transpose=True)
-
-        w_grp = const.tile([P, 4, P, 4], BF16, name="w_grp", align_bytes=64)
-        w_codes = const.tile([P, NH], U32, name="w_codes", align_bytes=64)
-        w_scales = const.tile([P, NH], U8, name="w_scales", align_bytes=64)
-        w_view = w_raw[:].rearrange("q t (m c) -> q c m t", c=4)
-        for c in (3, 0):
-            nc.vector.tensor_copy(out=w_grp[:, c], in_=w_view[:, c])
-        for c in (1, 2):
-            nc.scalar.copy(out=w_grp[:, c], in_=w_view[:, c])
-        for c in (3, 0, 1, 2):
-            nc.vector.quantize_mx(out=w_codes[:, c * P:(c + 1) * P].bitcast(FP8X4),
-                                  scales=w_scales[:, c * P:(c + 1) * P],
-                                  in_=w_grp[:, c].rearrange("q m t -> q (m t)"))
-        gate = const.tile([P, 4, NA], F32, name="gate")
-        gbias = const.tile([P, 4, NA], F32, name="gbias")
-        for c in range(4):
-            nc.vector.tensor_scalar(out=gate[:, c, :], in0=at_ps[:, c, :], scalar1=bcf[:, c:c + 1],
-                                    scalar2=None, op0=ALU.add)
-        f_codes = const.tile([P, NF], U32, name="f_codes", align_bytes=64)
-        f_scales = const.tile([P, NF], U8, name="f_scales", align_bytes=64)
 
         st = {}
 
@@ -136,12 +104,15 @@ def tile_dtnnstep_pa_t_kernel(tc, atom_features, distance_matrix, distance_matri
                 tps.append(tp)
             st[("t", q)] = tps
 
+        def evacuate_half(q, h, copy):
+            if h == 0:
+                st[("dg", q)] = work.tile([P, W * 4], BF16, name="d_grp", tag="d_grp", align_bytes=64)
+            g32 = st[("dg", q)][:].bitcast(F32).rearrange("p (h a i u) -> p h a i u", h=2, a=2, u=2)
+            copy(out=g32[:, h], in_=st[("t", q)][h][:].rearrange("p a u i -> p a i u"))
+
         def evacuate(q):
-            d_grp = work.tile([P, W * 4], BF16, name="d_grp", tag="d_grp", align_bytes=64)
-            g32 = d_grp[:].bitcast(F32).rearrange("p (h a i u) -> p h a i u", h=2, a=2, u=2)
             for h in range(2):
-                nc.scalar.copy(out=g32[:, h], in_=st[("t", q)][h][:].rearrange("p a u i -> p a i u"))
-            st[("dg", q)] = d_grp
+                evacuate_half(q, h, nc.scalar.copy)
 
         def quantise_d(q):
             d_codes = work.tile([P, W], U32, name="d_codes", tag="d_codes", align_bytes=64)
@@ -224,7 +195,57 @@ def tile_dtnnstep_pa_t_kernel(tc, atom_features, distance_matrix, distance_matri
         def live(q):
             return 0 <= q < NQ
 
-        for s in range(NQ + 7):
+        a32 = const.tile([P, NF], F32, name="a32")
+        nc.vector.tensor_copy(out=a32[:], in_=a_bf[:])
+        aT_ps = ps_1.tile([P, P], F32, name="aT_ps", tag="p1")
+        nc.tensor.transpose(aT_ps[:], a32[:], ident[:])
+        aT = const.tile([P, NA], BF16, name="aT")
+        nc.scalar.copy(out=aT[:], in_=aT_ps[:])
+        transposes(0)
+        load(LOADS_AHEAD)
+        evacuate_half(0, 0, nc.scalar.copy)
+        evacuate_half(0, 1, nc.vector.tensor_copy)
+        at_ps = ps_1.tile([P, 4, NA], F32, name="at_ps", tag="p1")
+        wcf = wcf_raw[:].rearrange("f (m c) -> f c m", c=4)
+        for c in range(4):
+            nc.tensor.matmul(at_ps[:, c, :], lhsT=wcf[:, c, :], rhs=aT[:], start=True, stop=True)
+        accT = ps_a.tile([P, NA], F32, name="accT")
+        nc.tensor.matmul(accT[:], lhsT=a32[:], rhs=ident[:], start=True, stop=False, is_transpose=True)
+        transposes(1)
+        load(LOADS_AHEAD + 1)
+
+        w_grp = const.tile([P, 4, P, 4], BF16, name="w_grp", align_bytes=64)
+        w_codes = const.tile([P, NH], U32, name="w_codes", align_bytes=64)
+        w_scales = const.tile([P, NH], U8, name="w_scales", align_bytes=64)
+        w_view = w_raw[:].rearrange("q t (m c) -> q c m t", c=4)
+
+        def quantise_w(c):
+            nc.vector.quantize_mx(out=w_codes[:, c * P:(c + 1) * P].bitcast(FP8X4),
+                                  scales=w_scales[:, c * P:(c + 1) * P],
+                                  in_=w_grp[:, c].rearrange("q m t -> q (m t)"))
+
+        gate = const.tile([P, 4, NA], F32, name="gate")
+        gbias = const.tile([P, 4, NA], F32, name="gbias")
+        nc.vector.tensor_tensor(out=gate[:], in0=at_ps[:], in1=bcf[:].unsqueeze(2).to_broadcast([P, 4, NA]),
+                                op=ALU.add)
+        for c in (3, 0):
+            nc.vector.tensor_copy(out=w_grp[:, c], in_=w_view[:, c])
+        for c in (1, 2):
+            nc.scalar.copy(out=w_grp[:, c], in_=w_view[:, c])
+        quantise_d(0)
+        quantise_w(3)
+        quantise_w(0)
+        nc.vector.tensor_tensor(out=gbias[:], in0=gate[:], in1=bdf[:].unsqueeze(2).to_broadcast([P, 4, NA]),
+                                op=ALU.mult)
+        evacuate_half(1, 0, nc.scalar.copy)
+        evacuate_half(1, 1, nc.vector.tensor_copy)
+        quantise_w(1)
+        quantise_w(2)
+        quantise_d(1)
+        f_codes = const.tile([P, NF], U32, name="f_codes", align_bytes=64)
+        f_scales = const.tile([P, NF], U8, name="f_scales", align_bytes=64)
+
+        for s in range(2, NQ + 7):
             q1 = s - 2
             passes = PASSES[q1 % 3] if live(q1) else ()
             if live(s - 4):
@@ -246,10 +267,6 @@ def tile_dtnnstep_pa_t_kernel(tc, atom_features, distance_matrix, distance_matri
                 tanh(s - 5)
             if live(s):
                 evacuate(s)
-            if s == 0:
-                for c in range(4):
-                    nc.scalar.activation(out=gbias[:, c, :], in_=gate[:, c, :], func=ACT.Copy,
-                                         scale=bdf[:, c:c + 1])
             if live(q1):
                 for c, eng in passes[2:4]:
                     mx1(q1, c)
@@ -265,7 +282,7 @@ def tile_dtnnstep_pa_t_kernel(tc, atom_features, distance_matrix, distance_matri
                 regroup(s - 3)
             if live(s):
                 quantise_d(s)
-            if s == 0:
+            if s == 2:
                 nc.vector.quantize_mx(out=f_codes[:].bitcast(FP8X4), scales=f_scales[:],
                                       in_=f_grp[:].rearrange("p f t -> p (f t)"))
 

@@ -24,10 +24,12 @@ W_VEC = 3 * W // 4
 FLOPS = 2 * NA * NA * ND * NH + 2 * NA * NA * NH * NF + 2 * NA * NF * NH
 
 PASSES = (
-    ((3, "v"), (0, "s"), (1, "s"), (2, "v")),
-    ((3, "v"), (0, "s"), (1, "s"), (2, "v")),
-    ((3, "v"), (0, "s"), (1, "s"), (2, "v")),
+    ((3, "v"), (2, "v"), (0, "s"), (1, "s")),
+    ((3, "v"), (2, "v"), (0, "s"), (1, "s")),
+    ((3, "v"), (2, "v"), (0, "s"), (1, "s")),
 )
+
+TAIL_PASSES = ((3, "v"), (0, "s"), (1, "s"), (2, "s"))
 
 
 def tile_dtnnstep_pa_t_kernel(tc, atom_features, distance_matrix, distance_matrix_mask,
@@ -83,11 +85,6 @@ def tile_dtnnstep_pa_t_kernel(tc, atom_features, distance_matrix, distance_matri
 
         ident = const.tile([P, P], F32, name="ident")
         make_identity(nc, ident[:])
-        f_grp = const.tile([P, NF, 4], BF16, name="f_grp", align_bytes=64)
-        nc.gpsimd.tensor_scalar(out=f_grp[:], in0=f_raw[:].rearrange("p t f -> p f t"), scalar1=1.0, scalar2=0.0,
-                                op0=ALU.mult, op1=ALU.add)
-        mask = const.tile([P, NA], F32, name="mask")
-        nc.gpsimd.tensor_scalar(out=mask[:], in0=m_bf[:], scalar1=1.0, scalar2=0.0, op0=ALU.mult, op1=ALU.add)
 
         st = {}
 
@@ -167,14 +164,17 @@ def tile_dtnnstep_pa_t_kernel(tc, atom_features, distance_matrix, distance_matri
                                   in_=st[("gg", q)][:].rearrange("p w t -> p (w t)"))
             st[("g", q)] = (g_codes, g_scales)
 
+        def mx2_one(p2, a, g_codes, g_scales, b):
+            nc.tensor.matmul_mx(out=p2[:, a, :], lhsT=g_codes[:, b * NA:(b + 1) * NA].bitcast(FP8X4),
+                                lhsT_scale=g_scales[:, b * NA:(b + 1) * NA],
+                                rhs=f_codes[:].bitcast(FP8X4), rhs_scale=f_scales[:],
+                                start=True, stop=True)
+
         def mx2(q):
             g_codes, g_scales = st[("g", q)]
             p2 = ps_2.tile([P, QJ, NF], F32, name="p2", tag="p2")
             for a in range(QJ):
-                nc.tensor.matmul_mx(out=p2[:, a, :], lhsT=g_codes[:, a * NA:(a + 1) * NA].bitcast(FP8X4),
-                                    lhsT_scale=g_scales[:, a * NA:(a + 1) * NA],
-                                    rhs=f_codes[:].bitcast(FP8X4), rhs_scale=f_scales[:],
-                                    start=True, stop=True)
+                mx2_one(p2, a, g_codes, g_scales, a)
             st[("p2", q)] = p2
 
         def tanh(q):
@@ -224,34 +224,38 @@ def tile_dtnnstep_pa_t_kernel(tc, atom_features, distance_matrix, distance_matri
                                   scales=w_scales[:, c * P:(c + 1) * P],
                                   in_=w_grp[:, c].rearrange("q m t -> q (m t)"))
 
+        f_grp = const.tile([P, NF, 4], BF16, name="f_grp", align_bytes=64)
         gate = const.tile([P, 4, NA], F32, name="gate")
         gbias = const.tile([P, 4, NA], F32, name="gbias")
-        nc.vector.tensor_tensor(out=gate[:], in0=at_ps[:], in1=bcf[:].unsqueeze(2).to_broadcast([P, 4, NA]),
-                                op=ALU.add)
-        for c in (3, 0):
-            nc.vector.tensor_copy(out=w_grp[:, c], in_=w_view[:, c])
-        for c in (1, 2):
+        for c in range(4):
+            nc.scalar.activation(out=gate[:, c, :], in_=at_ps[:, c, :], func=ACT.Identity, bias=bcf[:, c:c + 1])
+        nc.vector.tensor_copy(out=w_grp[:, 3], in_=w_view[:, 3])
+        for c in (0, 1):
             nc.scalar.copy(out=w_grp[:, c], in_=w_view[:, c])
         quantise_d(0)
         quantise_w(3)
-        quantise_w(0)
+        nc.vector.tensor_copy(out=w_grp[:, 2], in_=w_view[:, 2])
+        quantise_w(2)
         nc.vector.tensor_tensor(out=gbias[:], in0=gate[:], in1=bdf[:].unsqueeze(2).to_broadcast([P, 4, NA]),
                                 op=ALU.mult)
-        evacuate_half(1, 0, nc.scalar.copy)
-        evacuate_half(1, 1, nc.vector.tensor_copy)
+        quantise_w(0)
         quantise_w(1)
-        quantise_w(2)
+        nc.vector.tensor_copy(out=f_grp[:], in_=f_raw[:].rearrange("p t f -> p f t"))
+        evacuate(1)
         quantise_d(1)
+        mask = const.tile([P, NA], F32, name="mask")
         f_codes = const.tile([P, NF], U32, name="f_codes", align_bytes=64)
         f_scales = const.tile([P, NF], U8, name="f_scales", align_bytes=64)
 
-        for s in range(2, NQ + 7):
+        for s in range(2, NQ + 2):
             q1 = s - 2
-            passes = PASSES[q1 % 3] if live(q1) else ()
+            passes = PASSES[q1 % 3] if q1 < NQ - 2 else TAIL_PASSES
             if live(s - 4):
                 quantise_g(s - 4)
             if live(s - 3):
                 regroup_gpsimd(s - 3)
+            if s == 4:
+                nc.gpsimd.tensor_scalar(out=mask[:], in0=m_bf[:], scalar1=1.0, scalar2=0.0, op0=ALU.mult, op1=ALU.add)
             if live(q1):
                 planes = work.tile([P, 4, W], BF16, name="planes", tag="planes")
                 st[("pl", q1)] = planes
@@ -282,9 +286,40 @@ def tile_dtnnstep_pa_t_kernel(tc, atom_features, distance_matrix, distance_matri
                 regroup(s - 3)
             if live(s):
                 quantise_d(s)
-            if s == 2:
+            if s == 3:
                 nc.vector.quantize_mx(out=f_codes[:].bitcast(FP8X4), scales=f_scales[:],
                                       in_=f_grp[:].rearrange("p f t -> p (f t)"))
+
+        last = NQ - 1
+        HW = W // 2
+        halves = []
+        for h in range(2):
+            halves.append((const.tile([P, HW, 4], BF16, name=f"g_half{h}", align_bytes=64),
+                           const.tile([P, HW], U32, name=f"c_half{h}", align_bytes=64),
+                           const.tile([P, HW], U8, name=f"s_half{h}", align_bytes=64)))
+
+        def regroup_half(h, copy):
+            copy(out=halves[h][0][:].rearrange("p (x y) t -> p x t y", y=4),
+                 in_=st[("pl", last)][:, :, h * HW:(h + 1) * HW].rearrange("p t (x y) -> p x t y", y=4))
+
+        regroup_half(0, nc.vector.tensor_copy)
+        tanh(last - 2)
+        regroup_half(1, nc.scalar.copy)
+        quantise_g(last - 1)
+        for h in range(2):
+            nc.vector.quantize_mx(out=halves[h][1][:].bitcast(FP8X4), scales=halves[h][2][:],
+                                  in_=halves[h][0][:].rearrange("p w t -> p (w t)"))
+        add_up(last - 3)
+        mx2(last - 1)
+        tanh(last - 1)
+        p2 = ps_1.tile([P, QJ, NF], F32, name="p2_last", tag="p1")
+        for a in range(QJ):
+            mx2_one(p2, a, halves[a // 2][1], halves[a // 2][2], a % 2)
+        st[("p2", last)] = p2
+        tanh(last)
+        add_up(last - 2)
+        add_up(last - 1)
+        add_up(last)
 
         sumT = const.tile([P, NA], F32, name="sumT")
         nc.vector.tensor_copy(out=sumT[:], in_=accT[:])

@@ -20,7 +20,7 @@ QJ = 4
 NQ = NA // QJ
 W = QJ * NA
 LOADS_AHEAD = 6
-W_VEC = 3 * W // 4
+W_VEC = 11 * W // 16
 FLOPS = 2 * NA * NA * ND * NH + 2 * NA * NA * NH * NF + 2 * NA * NF * NH
 
 PASSES = (

@@ -44,7 +44,7 @@ def tile_dtnnstep_pa_t_kernel(tc, atom_features, distance_matrix, distance_matri
         const = ctx.enter_context(tc.tile_pool(name="const", bufs=1))
         dpool = ctx.enter_context(tc.tile_pool(name="dpool", bufs=LOADS_AHEAD))
         work = ctx.enter_context(tc.tile_pool(name="work", bufs=4))
-        gpool = ctx.enter_context(tc.tile_pool(name="gpool", bufs=1))
+        ring = ctx.enter_context(tc.tile_pool(name="ring", bufs=5))
         ps_t = ctx.enter_context(tc.psum_pool(name="ps_t", bufs=2))
         ps_1 = ctx.enter_context(tc.psum_pool(name="ps_1", bufs=4))
         ps_2 = ctx.enter_context(tc.psum_pool(name="ps_2", bufs=1))
@@ -147,10 +147,9 @@ def tile_dtnnstep_pa_t_kernel(tc, atom_features, distance_matrix, distance_matri
                 op0=ALU.add, op1=ALU.mult)
 
         def regroup_gpsimd(q):
-            g_grp = gpool.tile([P, W, 4], BF16, name="g_grp", tag="g_grp", align_bytes=64)
+            g_grp = st[("gg", q)]
             nc.gpsimd.tensor_scalar(out=g_grp[:, W_VEC:, :], in0=st[("pl", q)][:, :, W_VEC:].rearrange("p t w -> p w t"),
                                     scalar1=1.0, scalar2=0.0, op0=ALU.mult, op1=ALU.add)
-            st[("gg", q)] = g_grp
 
         def regroup(q):
             g_grp = st[("gg", q)]
@@ -170,9 +169,9 @@ def tile_dtnnstep_pa_t_kernel(tc, atom_features, distance_matrix, distance_matri
                                 rhs=f_codes[:].bitcast(FP8X4), rhs_scale=f_scales[:],
                                 start=True, stop=True)
 
-        def mx2(q):
+        def mx2(q, tail=False):
             g_codes, g_scales = st[("g", q)]
-            p2 = ps_2.tile([P, QJ, NF], F32, name="p2", tag="p2")
+            p2 = (ps_1 if tail else ps_2).tile([P, QJ, NF], F32, name="p2", tag="p1" if tail else "p2")
             for a in range(QJ):
                 mx2_one(p2, a, g_codes, g_scales, a)
             st[("p2", q)] = p2
@@ -250,42 +249,42 @@ def tile_dtnnstep_pa_t_kernel(tc, atom_features, distance_matrix, distance_matri
         for s in range(2, NQ + 2):
             q1 = s - 2
             passes = PASSES[q1 % 3] if q1 < NQ - 2 else TAIL_PASSES
-            if live(s - 4):
-                quantise_g(s - 4)
+            st[("pl", q1)] = ring.tile([P, 4, W], BF16, name="planes", tag="ring", align_bytes=64)
             if live(s - 3):
+                st[("gg", s - 3)] = ring.tile([P, W, 4], BF16, name="g_grp", tag="ring", align_bytes=64)
                 regroup_gpsimd(s - 3)
             if s == 4:
                 nc.gpsimd.tensor_scalar(out=mask[:], in0=m_bf[:], scalar1=1.0, scalar2=0.0, op0=ALU.mult, op1=ALU.add)
             if live(q1):
-                planes = work.tile([P, 4, W], BF16, name="planes", tag="planes")
-                st[("pl", q1)] = planes
                 for c, eng in passes[0:2]:
                     mx1(q1, c)
-            if live(s - 6):
-                add_up(s - 6)
+            if live(s - 7):
+                add_up(s - 7)
             if live(s):
                 transposes(s)
             if live(s + LOADS_AHEAD):
                 load(s + LOADS_AHEAD)
-            if live(s - 5):
-                tanh(s - 5)
+            if live(s - 6):
+                tanh(s - 6)
             if live(s):
                 evacuate(s)
             if live(q1):
                 for c, eng in passes[2:4]:
                     mx1(q1, c)
-            if live(s - 4):
-                mx2(s - 4)
+            if live(s - 5):
+                mx2(s - 5)
             for c, eng in passes:
                 if eng == "s":
                     gate_scalar(q1, c)
             vec = [c for c, eng in passes if eng == "v"]
             for c in vec:
                 gate_vector(q1, c)
-            if live(s - 3):
-                regroup(s - 3)
             if live(s):
                 quantise_d(s)
+            if live(s - 3):
+                regroup(s - 3)
+            if live(s - 4):
+                quantise_g(s - 4)
             if s == 3:
                 nc.vector.quantize_mx(out=f_codes[:].bitcast(FP8X4), scales=f_scales[:],
                                       in_=f_grp[:].rearrange("p f t -> p (f t)"))
@@ -302,15 +301,18 @@ def tile_dtnnstep_pa_t_kernel(tc, atom_features, distance_matrix, distance_matri
             copy(out=halves[h][0][:].rearrange("p (x y) t -> p x t y", y=4),
                  in_=st[("pl", last)][:, :, h * HW:(h + 1) * HW].rearrange("p t (x y) -> p x t y", y=4))
 
+        mx2(last - 2, tail=True)
         regroup_half(0, nc.vector.tensor_copy)
-        tanh(last - 2)
+        tanh(last - 3)
         regroup_half(1, nc.scalar.copy)
+        tanh(last - 2)
         quantise_g(last - 1)
         for h in range(2):
             nc.vector.quantize_mx(out=halves[h][1][:].bitcast(FP8X4), scales=halves[h][2][:],
                                   in_=halves[h][0][:].rearrange("p w t -> p (w t)"))
+        add_up(last - 4)
         add_up(last - 3)
-        mx2(last - 1)
+        mx2(last - 1, tail=True)
         tanh(last - 1)
         p2 = ps_1.tile([P, QJ, NF], F32, name="p2_last", tag="p1")
         for a in range(QJ):

@@ -20,7 +20,7 @@ QJ = 4
 NQ = NA // QJ
 W = QJ * NA
 LOADS_AHEAD = 6
-W_VEC = 11 * W // 16
+W_VEC = 5 * W // 8
 FLOPS = 2 * NA * NA * ND * NH + 2 * NA * NA * NH * NF + 2 * NA * NF * NH
 
 PASSES = (

@@ -19,6 +19,7 @@ NF = 128
 QJ = 4
 NQ = NA // QJ
 W = QJ * NA
+W_VEC_LAST = 13 * W // 16
 LOADS_AHEAD = 6
 W_VEC = 5 * W // 8
 FLOPS = 2 * NA * NA * ND * NH + 2 * NA * NA * NH * NF + 2 * NA * NF * NH
@@ -88,6 +89,9 @@ def tile_dtnnstep_pa_t_kernel(tc, atom_features, distance_matrix, distance_matri
 
         st = {}
 
+        def live(q):
+            return 0 <= q < NQ
+
         def transposes(q):
             d32 = dtiles[q][:].bitcast(F32)
             tps = []
@@ -102,66 +106,75 @@ def tile_dtnnstep_pa_t_kernel(tc, atom_features, distance_matrix, distance_matri
             st[("t", q)] = tps
 
         def evacuate_half(q, h, copy):
-            if h == 0:
-                st[("dg", q)] = work.tile([P, W * 4], BF16, name="d_grp", tag="d_grp", align_bytes=64)
-            g32 = st[("dg", q)][:].bitcast(F32).rearrange("p (h a i u) -> p h a i u", h=2, a=2, u=2)
+            g32 = st[("x", q)][:, 0].bitcast(F32).rearrange("p (h a i u) -> p h a i u", h=2, a=2, u=2)
             copy(out=g32[:, h], in_=st[("t", q)][h][:].rearrange("p a u i -> p a i u"))
 
         def evacuate(q):
             for h in range(2):
                 evacuate_half(q, h, nc.scalar.copy)
 
-        def quantise_d(q):
-            d_codes = work.tile([P, W], U32, name="d_codes", tag="d_codes", align_bytes=64)
-            d_scales = work.tile([P, W], U8, name="d_scales", tag="d_scales", align_bytes=64)
-            nc.vector.quantize_mx(out=d_codes[:].bitcast(FP8X4), scales=d_scales[:], in_=st[("dg", q)][:])
-            st[("d", q)] = (d_codes, d_scales)
+        def new_x(k):
+            st[("x", k)] = ring.tile([P, 2, 4 * W], BF16, name="x", tag="ring", align_bytes=64)
+
+        def grouped(q):
+            return st[("x", q + 4)][:, 1].rearrange("p (w t) -> p w t", t=4)
+
+        def planes(q):
+            return st[("pl", q)][:, 1].rearrange("p (t w) -> p t w", t=4)
+
+        def quantise(k):
+            lo = 0 if live(k) else 1
+            hi = 2 if live(k - 4) else 1
+            codes = work.tile([P, 2 * W], U32, name="codes", tag="codes", align_bytes=64)
+            scales = work.tile([P, 2 * W], U8, name="scales", tag="scales", align_bytes=64)
+            nc.vector.quantize_mx(out=codes[:, lo * W:hi * W].bitcast(FP8X4), scales=scales[:, lo * W:hi * W],
+                                  in_=st[("x", k)][:, lo:hi].rearrange("p b n -> p (b n)"))
+            st[("c", k)] = (codes, scales)
 
         def mx1(q, c):
-            d_codes, d_scales = st[("d", q)]
+            codes, scales = st[("c", q)]
+            d_codes, d_scales = codes[:, :W], scales[:, :W]
             p1 = ps_1.tile([P, W], F32, name="p1", tag="p1")
             nc.tensor.matmul_mx(out=p1[:], lhsT=w_codes[:, c * P:(c + 1) * P].bitcast(FP8X4),
                                 lhsT_scale=w_scales[:, c * P:(c + 1) * P],
-                                rhs=d_codes[:].bitcast(FP8X4), rhs_scale=d_scales[:],
+                                rhs=d_codes.bitcast(FP8X4), rhs_scale=d_scales,
                                 start=True, stop=True)
             st[("p1", q, c)] = p1
 
         def gate_scalar(q, c):
             p1 = st[("p1", q, c)]
-            planes = st[("pl", q)]
+            pl = planes(q)
             j0 = q * QJ
             for a in range(QJ):
-                nc.scalar.activation(out=planes[:, c, a * NA:(a + 1) * NA], in_=p1[:, a * NA:(a + 1) * NA],
+                nc.scalar.activation(out=pl[:, c, a * NA:(a + 1) * NA], in_=p1[:, a * NA:(a + 1) * NA],
                                      func=ACT.Identity, scale=gate[:, c, j0 + a:j0 + a + 1],
                                      bias=gbias[:, c, j0 + a:j0 + a + 1])
 
         def gate_vector(q, c):
             p1 = st[("p1", q, c)]
-            planes = st[("pl", q)]
+            pl = planes(q)
             j0 = q * QJ
             nc.vector.scalar_tensor_tensor(
-                out=planes[:, c, :].rearrange("p (a i) -> p a i", a=QJ),
+                out=pl[:, c, :].rearrange("p (a i) -> p a i", a=QJ),
                 in0=p1[:].rearrange("p (a i) -> p a i", a=QJ),
                 scalar=bdf[:, c:c + 1],
                 in1=gate[:, c, j0:j0 + QJ].unsqueeze(2).to_broadcast([P, QJ, NA]),
                 op0=ALU.add, op1=ALU.mult)
 
+        def w_vec(q):
+            return W_VEC if q < NQ - 3 else W_VEC_LAST
+
         def regroup_gpsimd(q):
-            g_grp = st[("gg", q)]
-            nc.gpsimd.tensor_scalar(out=g_grp[:, W_VEC:, :], in0=st[("pl", q)][:, :, W_VEC:].rearrange("p t w -> p w t"),
+            g_grp = grouped(q)
+            n = w_vec(q)
+            nc.gpsimd.tensor_scalar(out=g_grp[:, n:, :], in0=planes(q)[:, :, n:].rearrange("p t w -> p w t"),
                                     scalar1=1.0, scalar2=0.0, op0=ALU.mult, op1=ALU.add)
 
         def regroup(q):
-            g_grp = st[("gg", q)]
-            nc.vector.tensor_copy(out=g_grp[:, :W_VEC, :].rearrange("p (x y) t -> p x t y", y=4),
-                                  in_=st[("pl", q)][:, :, :W_VEC].rearrange("p t (x y) -> p x t y", y=4))
-
-        def quantise_g(q):
-            g_codes = work.tile([P, W], U32, name="g_codes", tag="g_codes", align_bytes=64)
-            g_scales = work.tile([P, W], U8, name="g_scales", tag="g_scales", align_bytes=64)
-            nc.vector.quantize_mx(out=g_codes[:].bitcast(FP8X4), scales=g_scales[:],
-                                  in_=st[("gg", q)][:].rearrange("p w t -> p (w t)"))
-            st[("g", q)] = (g_codes, g_scales)
+            g_grp = grouped(q)
+            n = w_vec(q)
+            nc.vector.tensor_copy(out=g_grp[:, :n, :].rearrange("p (x y) t -> p x t y", y=4),
+                                  in_=planes(q)[:, :, :n].rearrange("p t (x y) -> p x t y", y=4))
 
         def mx2_one(p2, a, g_codes, g_scales, b):
             nc.tensor.matmul_mx(out=p2[:, a, :], lhsT=g_codes[:, b * NA:(b + 1) * NA].bitcast(FP8X4),
@@ -170,7 +183,8 @@ def tile_dtnnstep_pa_t_kernel(tc, atom_features, distance_matrix, distance_matri
                                 start=True, stop=True)
 
         def mx2(q, tail=False):
-            g_codes, g_scales = st[("g", q)]
+            codes, scales = st[("c", q + 4)]
+            g_codes, g_scales = codes[:, W:], scales[:, W:]
             p2 = (ps_1 if tail else ps_2).tile([P, QJ, NF], F32, name="p2", tag="p1" if tail else "p2")
             for a in range(QJ):
                 mx2_one(p2, a, g_codes, g_scales, a)
@@ -191,15 +205,14 @@ def tile_dtnnstep_pa_t_kernel(tc, atom_features, distance_matrix, distance_matri
                 nc.tensor.matmul(accT[:], lhsT=th[:, a, :], rhs=ident[:], start=False,
                                  stop=(q == NQ - 1 and a == QJ - 1), is_transpose=True)
 
-        def live(q):
-            return 0 <= q < NQ
-
         a32 = const.tile([P, NF], F32, name="a32")
         nc.vector.tensor_copy(out=a32[:], in_=a_bf[:])
         aT_ps = ps_1.tile([P, P], F32, name="aT_ps", tag="p1")
         nc.tensor.transpose(aT_ps[:], a32[:], ident[:])
         aT = const.tile([P, NA], BF16, name="aT")
         nc.scalar.copy(out=aT[:], in_=aT_ps[:])
+        new_x(0)
+        new_x(1)
         transposes(0)
         load(LOADS_AHEAD)
         evacuate_half(0, 0, nc.scalar.copy)
@@ -231,7 +244,7 @@ def tile_dtnnstep_pa_t_kernel(tc, atom_features, distance_matrix, distance_matri
         nc.vector.tensor_copy(out=w_grp[:, 3], in_=w_view[:, 3])
         for c in (0, 1):
             nc.scalar.copy(out=w_grp[:, c], in_=w_view[:, c])
-        quantise_d(0)
+        quantise(0)
         quantise_w(3)
         nc.vector.tensor_copy(out=w_grp[:, 2], in_=w_view[:, 2])
         quantise_w(2)
@@ -241,27 +254,27 @@ def tile_dtnnstep_pa_t_kernel(tc, atom_features, distance_matrix, distance_matri
         quantise_w(1)
         nc.vector.tensor_copy(out=f_grp[:], in_=f_raw[:].rearrange("p t f -> p f t"))
         evacuate(1)
-        quantise_d(1)
         mask = const.tile([P, NA], F32, name="mask")
+        nc.scalar.copy(out=mask[:], in_=m_bf[:])
+        quantise(1)
+        new_x(2)
         f_codes = const.tile([P, NF], U32, name="f_codes", align_bytes=64)
         f_scales = const.tile([P, NF], U8, name="f_scales", align_bytes=64)
 
         for s in range(2, NQ + 2):
             q1 = s - 2
             passes = PASSES[q1 % 3] if q1 < NQ - 2 else TAIL_PASSES
-            st[("pl", q1)] = ring.tile([P, 4, W], BF16, name="planes", tag="ring", align_bytes=64)
+            st[("pl", q1)] = ring.tile([P, 2, 4 * W], BF16, name="planes", tag="ring", align_bytes=64)
+            new_x(s + 1)
             if live(s - 3):
-                st[("gg", s - 3)] = ring.tile([P, W, 4], BF16, name="g_grp", tag="ring", align_bytes=64)
                 regroup_gpsimd(s - 3)
-            if s == 4:
-                nc.gpsimd.tensor_scalar(out=mask[:], in0=m_bf[:], scalar1=1.0, scalar2=0.0, op0=ALU.mult, op1=ALU.add)
             if live(q1):
                 for c, eng in passes[0:2]:
                     mx1(q1, c)
-            if live(s - 7):
-                add_up(s - 7)
             if live(s):
                 transposes(s)
+            if live(s - 7):
+                add_up(s - 7)
             if live(s + LOADS_AHEAD):
                 load(s + LOADS_AHEAD)
             if live(s - 6):
@@ -279,12 +292,9 @@ def tile_dtnnstep_pa_t_kernel(tc, atom_features, distance_matrix, distance_matri
             vec = [c for c, eng in passes if eng == "v"]
             for c in vec:
                 gate_vector(q1, c)
-            if live(s):
-                quantise_d(s)
             if live(s - 3):
                 regroup(s - 3)
-            if live(s - 4):
-                quantise_g(s - 4)
+            quantise(s)
             if s == 3:
                 nc.vector.quantize_mx(out=f_codes[:].bitcast(FP8X4), scales=f_scales[:],
                                       in_=f_grp[:].rearrange("p f t -> p (f t)"))
@@ -299,14 +309,14 @@ def tile_dtnnstep_pa_t_kernel(tc, atom_features, distance_matrix, distance_matri
 
         def regroup_half(h, copy):
             copy(out=halves[h][0][:].rearrange("p (x y) t -> p x t y", y=4),
-                 in_=st[("pl", last)][:, :, h * HW:(h + 1) * HW].rearrange("p t (x y) -> p x t y", y=4))
+                 in_=planes(last)[:, :, h * HW:(h + 1) * HW].rearrange("p t (x y) -> p x t y", y=4))
 
         mx2(last - 2, tail=True)
         regroup_half(0, nc.vector.tensor_copy)
         tanh(last - 3)
         regroup_half(1, nc.scalar.copy)
         tanh(last - 2)
-        quantise_g(last - 1)
+        quantise(last + 3)
         for h in range(2):
             nc.vector.quantize_mx(out=halves[h][1][:].bitcast(FP8X4), scales=halves[h][2][:],
                                   in_=halves[h][0][:].rearrange("p w t -> p (w t)"))

@@ -182,13 +182,13 @@ def tile_dtnnstep_pa_t_kernel(tc, atom_features, distance_matrix, distance_matri
                                 rhs=f_codes[:].bitcast(FP8X4), rhs_scale=f_scales[:],
                                 start=True, stop=True)
 
-        def mx2(q, tail=False):
+        def mx2(q, js, tail=False):
             codes, scales = st[("c", q + 4)]
             g_codes, g_scales = codes[:, W:], scales[:, W:]
-            p2 = (ps_1 if tail else ps_2).tile([P, QJ, NF], F32, name="p2", tag="p1" if tail else "p2")
-            for a in range(QJ):
-                mx2_one(p2, a, g_codes, g_scales, a)
-            st[("p2", q)] = p2
+            if js[0] == 0:
+                st[("p2", q)] = (ps_1 if tail else ps_2).tile([P, QJ, NF], F32, name="p2", tag="p1" if tail else "p2")
+            for a in js:
+                mx2_one(st[("p2", q)], a, g_codes, g_scales, a)
 
         def tanh(q):
             p2 = st[("p2", q)]
@@ -268,9 +268,10 @@ def tile_dtnnstep_pa_t_kernel(tc, atom_features, distance_matrix, distance_matri
             new_x(s + 1)
             if live(s - 3):
                 regroup_gpsimd(s - 3)
-            if live(q1):
-                for c, eng in passes[0:2]:
-                    mx1(q1, c)
+            mx1(q1, passes[0][0])
+            if live(s - 6):
+                mx2(s - 6, (2, 3))
+            mx1(q1, passes[1][0])
             if live(s):
                 transposes(s)
             if live(s - 7):
@@ -285,7 +286,7 @@ def tile_dtnnstep_pa_t_kernel(tc, atom_features, distance_matrix, distance_matri
                 for c, eng in passes[2:4]:
                     mx1(q1, c)
             if live(s - 5):
-                mx2(s - 5)
+                mx2(s - 5, (0, 1))
             for c, eng in passes:
                 if eng == "s":
                     gate_scalar(q1, c)
@@ -311,7 +312,8 @@ def tile_dtnnstep_pa_t_kernel(tc, atom_features, distance_matrix, distance_matri
             copy(out=halves[h][0][:].rearrange("p (x y) t -> p x t y", y=4),
                  in_=planes(last)[:, :, h * HW:(h + 1) * HW].rearrange("p t (x y) -> p x t y", y=4))
 
-        mx2(last - 2, tail=True)
+        mx2(last - 3, (2, 3))
+        mx2(last - 2, range(QJ), tail=True)
         regroup_half(0, nc.vector.tensor_copy)
         tanh(last - 3)
         regroup_half(1, nc.scalar.copy)
@@ -322,7 +324,7 @@ def tile_dtnnstep_pa_t_kernel(tc, atom_features, distance_matrix, distance_matri
                                   in_=halves[h][0][:].rearrange("p w t -> p (w t)"))
         add_up(last - 4)
         add_up(last - 3)
-        mx2(last - 1, tail=True)
+        mx2(last - 1, range(QJ), tail=True)
         tanh(last - 1)
         p2 = ps_1.tile([P, QJ, NF], F32, name="p2_last", tag="p1")
         for a in range(QJ):

@@ -92,22 +92,23 @@ def tile_dtnnstep_pa_t_kernel(tc, atom_features, distance_matrix, distance_matri
         def live(q):
             return 0 <= q < NQ
 
-        def transposes(q):
+        def transposes_half(q, h):
             d32 = dtiles[q][:].bitcast(F32)
-            tps = []
+            tp = ps_t.tile([P, 2, 2, NA], F32, name="tp", tag="tp")
+            for a in range(2):
+                jj = 2 * h + a
+                for u in range(2):
+                    nc.tensor.transpose(tp[:, a, u, :], d32[:, jj * 256 + u * P:jj * 256 + (u + 1) * P],
+                                        ident[:])
+            st[("t", q, h)] = tp
+
+        def transposes(q):
             for h in range(2):
-                tp = ps_t.tile([P, 2, 2, NA], F32, name="tp", tag="tp")
-                for a in range(2):
-                    jj = 2 * h + a
-                    for u in range(2):
-                        nc.tensor.transpose(tp[:, a, u, :], d32[:, jj * 256 + u * P:jj * 256 + (u + 1) * P],
-                                            ident[:])
-                tps.append(tp)
-            st[("t", q)] = tps
+                transposes_half(q, h)
 
         def evacuate_half(q, h, copy):
             g32 = st[("x", q)][:, 0].bitcast(F32).rearrange("p (h a i u) -> p h a i u", h=2, a=2, u=2)
-            copy(out=g32[:, h], in_=st[("t", q)][h][:].rearrange("p a u i -> p a i u"))
+            copy(out=g32[:, h], in_=st[("t", q, h)][:].rearrange("p a u i -> p a i u"))
 
         def evacuate(q):
             for h in range(2):
@@ -205,15 +206,26 @@ def tile_dtnnstep_pa_t_kernel(tc, atom_features, distance_matrix, distance_matri
                 nc.tensor.matmul(accT[:], lhsT=th[:, a, :], rhs=ident[:], start=False,
                                  stop=(q == NQ - 1 and a == QJ - 1), is_transpose=True)
 
+        zeros = const.tile([P, W], BF16, name="zeros")
+        nc.vector.memset(zeros[:], 0.0)
+        warm_ps = ps_2.tile([P, W], F32, name="warm_ps", tag="p2")
+
+        def warm_up(n):
+            for k in range(n):
+                nc.tensor.matmul(warm_ps[:], lhsT=zeros[:, :P], rhs=zeros[:], start=True, stop=True)
+
         a32 = const.tile([P, NF], F32, name="a32")
         nc.vector.tensor_copy(out=a32[:], in_=a_bf[:])
+        warm_up(4)
         aT_ps = ps_1.tile([P, P], F32, name="aT_ps", tag="p1")
         nc.tensor.transpose(aT_ps[:], a32[:], ident[:])
         aT = const.tile([P, NA], BF16, name="aT")
         nc.scalar.copy(out=aT[:], in_=aT_ps[:])
         new_x(0)
         new_x(1)
-        transposes(0)
+        transposes_half(0, 0)
+        warm_up(2)
+        transposes_half(0, 1)
         load(LOADS_AHEAD)
         evacuate_half(0, 0, nc.scalar.copy)
         evacuate_half(0, 1, nc.vector.tensor_copy)
@@ -223,6 +235,7 @@ def tile_dtnnstep_pa_t_kernel(tc, atom_features, distance_matrix, distance_matri
             nc.tensor.matmul(at_ps[:, c, :], lhsT=wcf[:, c, :], rhs=aT[:], start=True, stop=True)
         accT = ps_a.tile([P, NA], F32, name="accT")
         nc.tensor.matmul(accT[:], lhsT=a32[:], rhs=ident[:], start=True, stop=False, is_transpose=True)
+        warm_up(4)
         transposes(1)
         load(LOADS_AHEAD + 1)
 

@@ -21,7 +21,7 @@ NQ = NA // QJ
 W = QJ * NA
 W_VEC_LAST = 13 * W // 16
 LOADS_AHEAD = 6
-W_VEC = 5 * W // 8
+W_VEC = 19 * W // 32
 FLOPS = 2 * NA * NA * ND * NH + 2 * NA * NA * NH * NF + 2 * NA * NF * NH
 
 PASSES = (
@@ -168,7 +168,8 @@ def tile_dtnnstep_pa_t_kernel(tc, atom_features, distance_matrix, distance_matri
         def regroup_gpsimd(q):
             g_grp = grouped(q)
             n = w_vec(q)
-            nc.gpsimd.tensor_scalar(out=g_grp[:, n:, :], in0=planes(q)[:, :, n:].rearrange("p t w -> p w t"),
+            nc.gpsimd.tensor_scalar(out=g_grp[:, n:, :].rearrange("p (x y) t -> p x t y", y=4),
+                                    in0=planes(q)[:, :, n:].rearrange("p t (x y) -> p x t y", y=4),
                                     scalar1=1.0, scalar2=0.0, op0=ALU.mult, op1=ALU.add)
 
         def regroup(q):

from contextlib import ExitStack

import concourse.mybir as mybir
from concourse.masks import make_identity

F32 = mybir.dt.float32
BF16 = mybir.dt.bfloat16
U32 = mybir.dt.uint32
U8 = mybir.dt.uint8
FP8X4 = mybir.dt.float8_e4m3fn_x4
ALU = mybir.AluOpType
ACT = mybir.ActivationFunctionType

P = 128
NA = 128
ND = 512
NH = 512
NF = 128
QJ = 4
NQ = NA // QJ
W = QJ * NA
W_VEC_LAST = 13 * W // 16
LOADS_AHEAD = 6
W_VEC = 19 * W // 32
FLOPS = 2 * NA * NA * ND * NH + 2 * NA * NA * NH * NF + 2 * NA * NF * NH

PASSES = (
    ((3, "v"), (2, "v"), (0, "s"), (1, "s")),
    ((3, "v"), (2, "v"), (0, "s"), (1, "s")),
    ((3, "v"), (2, "v"), (0, "s"), (1, "s")),
)

TAIL_PASSES = ((3, "v"), (0, "s"), (1, "s"), (2, "s"))


def tile_dtnnstep_pa_t_kernel(tc, atom_features, distance_matrix, distance_matrix_mask,
                                         W_cf, W_df, W_fc, b_cf, b_df, out):
    nc = tc.nc
    a_dram = atom_features.rearrange("b j f -> (b j) f")
    d_dram = distance_matrix.rearrange("b i j k -> (b i) (j k)")
    m_dram = distance_matrix_mask.rearrange("b i j -> (b i) j")
    o_dram = out.rearrange("b i f -> (b i) f")

    with ExitStack() as ctx:
        const = ctx.enter_context(tc.tile_pool(name="const", bufs=1))
        dpool = ctx.enter_context(tc.tile_pool(name="dpool", bufs=LOADS_AHEAD))
        work = ctx.enter_context(tc.tile_pool(name="work", bufs=4))
        ring = ctx.enter_context(tc.tile_pool(name="ring", bufs=5))
        ps_t = ctx.enter_context(tc.psum_pool(name="ps_t", bufs=2))
        ps_1 = ctx.enter_context(tc.psum_pool(name="ps_1", bufs=4))
        ps_2 = ctx.enter_context(tc.psum_pool(name="ps_2", bufs=1))
        ps_a = ctx.enter_context(tc.psum_pool(name="ps_a", bufs=1))
        ctx.enter_context(tc.manual_schedule())

        dtiles = {}

        def load(q, pieces=1):
            dt_ = dpool.tile([P, QJ * ND], BF16, name="dt_", tag="dt_")
            n = QJ * ND // pieces
            for u in range(pieces):
                nc.sync.dma_start(out=dt_[:, u * n:(u + 1) * n],
                                  in_=d_dram[:, q * QJ * ND + u * n:q * QJ * ND + (u + 1) * n])
            dtiles[q] = dt_

        a_bf = const.tile([P, NF], BF16, name="a_bf")
        nc.scalar.dma_start(out=a_bf[:], in_=a_dram)
        wcf_raw = const.tile([P, NH], BF16, name="wcf_raw")
        nc.scalar.dma_start(out=wcf_raw[:], in_=W_cf)
        load(0, pieces=2)
        w_raw = const.tile([P, 4, NH], BF16, name="w_raw")
        for u in range(2):
            nc.sync.dma_start(out=w_raw[:, 2 * u:2 * u + 2, :],
                              in_=W_df[256 * u:256 * u + 256, :].rearrange("(q e) h -> q e h", e=2))
        bcf = const.tile([P, 4], BF16, name="bcf")
        nc.scalar.dma_start(out=bcf[:], in_=b_cf.rearrange("(m c) -> m c", c=4))
        bdf = const.tile([P, 4], BF16, name="bdf")
        nc.scalar.dma_start(out=bdf[:], in_=b_df.rearrange("(m c) -> m c", c=4))
        load(1)
        load(2)
        f_raw = const.tile([P, 4, NF], BF16, name="f_raw")
        nc.sync.dma_start(out=f_raw[:], in_=W_fc.rearrange("(p t) f -> p t f", t=4))
        m_bf = const.tile([P, NA], BF16, name="m_bf")
        nc.sync.dma_start(out=m_bf[:], in_=m_dram)
        for q in range(3, LOADS_AHEAD):
            load(q)

        ident = const.tile([P, P], F32, name="ident")
        make_identity(nc, ident[:])

        st = {}

        def live(q):
            return 0 <= q < NQ

        def transposes_half(q, h):
            d32 = dtiles[q][:].bitcast(F32)
            tp = ps_t.tile([P, 2, 2, NA], F32, name="tp", tag="tp")
            for a in range(2):
                jj = 2 * h + a
                for u in range(2):
                    nc.tensor.transpose(tp[:, a, u, :], d32[:, jj * 256 + u * P:jj * 256 + (u + 1) * P],
                                        ident[:])
            st[("t", q, h)] = tp

        def transposes(q):
            for h in range(2):
                transposes_half(q, h)

        def evacuate_half(q, h, copy):
            g32 = st[("x", q)][:, 0].bitcast(F32).rearrange("p (h a i u) -> p h a i u", h=2, a=2, u=2)
            copy(out=g32[:, h], in_=st[("t", q, h)][:].rearrange("p a u i -> p a i u"))

        def evacuate(q):
            for h in range(2):
                evacuate_half(q, h, nc.scalar.copy)

        def new_x(k):
            st[("x", k)] = ring.tile([P, 2, 4 * W], BF16, name="x", tag="ring", align_bytes=64)

        def grouped(q):
            return st[("x", q + 4)][:, 1].rearrange("p (w t) -> p w t", t=4)

        def planes(q):
            return st[("pl", q)][:, 1].rearrange("p (t w) -> p t w", t=4)

        def quantise(k):
            lo = 0 if live(k) else 1
            hi = 2 if live(k - 4) else 1
            codes = work.tile([P, 2 * W], U32, name="codes", tag="codes", align_bytes=64)
            scales = work.tile([P, 2 * W], U8, name="scales", tag="scales", align_bytes=64)
            nc.vector.quantize_mx(out=codes[:, lo * W:hi * W].bitcast(FP8X4), scales=scales[:, lo * W:hi * W],
                                  in_=st[("x", k)][:, lo:hi].rearrange("p b n -> p (b n)"))
            st[("c", k)] = (codes, scales)

        def mx1(q, c):
            codes, scales = st[("c", q)]
            d_codes, d_scales = codes[:, :W], scales[:, :W]
            p1 = ps_1.tile([P, W], F32, name="p1", tag="p1")
            nc.tensor.matmul_mx(out=p1[:], lhsT=w_codes[:, c * P:(c + 1) * P].bitcast(FP8X4),
                                lhsT_scale=w_scales[:, c * P:(c + 1) * P],
                                rhs=d_codes.bitcast(FP8X4), rhs_scale=d_scales,
                                start=True, stop=True)
            st[("p1", q, c)] = p1

        def gate_scalar(q, c):
            p1 = st[("p1", q, c)]
            pl = planes(q)
            j0 = q * QJ
            for a in range(QJ):
                nc.scalar.activation(out=pl[:, c, a * NA:(a + 1) * NA], in_=p1[:, a * NA:(a + 1) * NA],
                                     func=ACT.Identity, scale=gate[:, c, j0 + a:j0 + a + 1],
                                     bias=gbias[:, c, j0 + a:j0 + a + 1])

        def gate_vector(q, c):
            p1 = st[("p1", q, c)]
            pl = planes(q)
            j0 = q * QJ
            nc.vector.scalar_tensor_tensor(
                out=pl[:, c, :].rearrange("p (a i) -> p a i", a=QJ),
                in0=p1[:].rearrange("p (a i) -> p a i", a=QJ),
                scalar=bdf[:, c:c + 1],
                in1=gate[:, c, j0:j0 + QJ].unsqueeze(2).to_broadcast([P, QJ, NA]),
                op0=ALU.add, op1=ALU.mult)

        def w_vec(q):
            return W_VEC if q < NQ - 3 else W_VEC_LAST

        def regroup_gpsimd(q):
            g_grp = grouped(q)
            n = w_vec(q)
            nc.gpsimd.tensor_scalar(out=g_grp[:, n:, :].rearrange("p (x y) t -> p x t y", y=4),
                                    in0=planes(q)[:, :, n:].rearrange("p t (x y) -> p x t y", y=4),
                                    scalar1=1.0, scalar2=0.0, op0=ALU.mult, op1=ALU.add)

        def regroup(q):
            g_grp = grouped(q)
            n = w_vec(q)
            nc.vector.tensor_copy(out=g_grp[:, :n, :].rearrange("p (x y) t -> p x t y", y=4),
                                  in_=planes(q)[:, :, :n].rearrange("p t (x y) -> p x t y", y=4))

        def mx2_one(p2, a, g_codes, g_scales, b):
            nc.tensor.matmul_mx(out=p2[:, a, :], lhsT=g_codes[:, b * NA:(b + 1) * NA].bitcast(FP8X4),
                                lhsT_scale=g_scales[:, b * NA:(b + 1) * NA],
                                rhs=f_codes[:].bitcast(FP8X4), rhs_scale=f_scales[:],
                                start=True, stop=True)

        def mx2(q, js, tail=False):
            codes, scales = st[("c", q + 4)]
            g_codes, g_scales = codes[:, W:], scales[:, W:]
            if js[0] == 0:
                st[("p2", q)] = (ps_1 if tail else ps_2).tile([P, QJ, NF], F32, name="p2", tag="p1" if tail else "p2")
            for a in js:
                mx2_one(st[("p2", q)], a, g_codes, g_scales, a)

        def tanh(q):
            p2 = st[("p2", q)]
            j0 = q * QJ
            th = work.tile([P, QJ, NF], F32, name="th", tag="th")
            for a in range(QJ):
                nc.scalar.activation(out=th[:, a, :], in_=p2[:, a, :], func=ACT.Tanh,
                                     scale=mask[:, j0 + a:j0 + a + 1])
            st[("th", q)] = th

        def add_up(q):
            th = st[("th", q)]
            for a in range(QJ):
                nc.tensor.matmul(accT[:], lhsT=th[:, a, :], rhs=ident[:], start=False,
                                 stop=(q == NQ - 1 and a == QJ - 1), is_transpose=True)

        zeros = const.tile([P, W], BF16, name="zeros")
        nc.vector.memset(zeros[:], 0.0)
        warm_ps = ps_2.tile([P, W], F32, name="warm_ps", tag="p2")

        def warm_up(n):
            for k in range(n):
                nc.tensor.matmul(warm_ps[:], lhsT=zeros[:, :P], rhs=zeros[:], start=True, stop=True)

        a32 = const.tile([P, NF], F32, name="a32")
        nc.vector.tensor_copy(out=a32[:], in_=a_bf[:])
        warm_up(4)
        aT_ps = ps_1.tile([P, P], F32, name="aT_ps", tag="p1")
        nc.tensor.transpose(aT_ps[:], a32[:], ident[:])
        aT = const.tile([P, NA], BF16, name="aT")
        nc.scalar.copy(out=aT[:], in_=aT_ps[:])
        new_x(0)
        new_x(1)
        transposes_half(0, 0)
        warm_up(2)
        transposes_half(0, 1)
        load(LOADS_AHEAD)
        evacuate_half(0, 0, nc.scalar.copy)
        evacuate_half(0, 1, nc.vector.tensor_copy)
        at_ps = ps_1.tile([P, 4, NA], F32, name="at_ps", tag="p1")
        wcf = wcf_raw[:].rearrange("f (m c) -> f c m", c=4)
        for c in range(4):
            nc.tensor.matmul(at_ps[:, c, :], lhsT=wcf[:, c, :], rhs=aT[:], start=True, stop=True)
        accT = ps_a.tile([P, NA], F32, name="accT")
        nc.tensor.matmul(accT[:], lhsT=a32[:], rhs=ident[:], start=True, stop=False, is_transpose=True)
        warm_up(4)
        transposes(1)
        load(LOADS_AHEAD + 1)

        w_grp = const.tile([P, 4, P, 4], BF16, name="w_grp", align_bytes=64)
        w_codes = const.tile([P, NH], U32, name="w_codes", align_bytes=64)
        w_scales = const.tile([P, NH], U8, name="w_scales", align_bytes=64)
        w_view = w_raw[:].rearrange("q t (m c) -> q c m t", c=4)

        def quantise_w(c):
            nc.vector.quantize_mx(out=w_codes[:, c * P:(c + 1) * P].bitcast(FP8X4),
                                  scales=w_scales[:, c * P:(c + 1) * P],
                                  in_=w_grp[:, c].rearrange("q m t -> q (m t)"))

        f_grp = const.tile([P, NF, 4], BF16, name="f_grp", align_bytes=64)
        gate = const.tile([P, 4, NA], F32, name="gate")
        gbias = const.tile([P, 4, NA], F32, name="gbias")
        for c in range(4):
            nc.scalar.activation(out=gate[:, c, :], in_=at_ps[:, c, :], func=ACT.Identity, bias=bcf[:, c:c + 1])
        nc.vector.tensor_copy(out=w_grp[:, 3], in_=w_view[:, 3])
        for c in (0, 1):
            nc.scalar.copy(out=w_grp[:, c], in_=w_view[:, c])
        quantise(0)
        quantise_w(3)
        nc.vector.tensor_copy(out=w_grp[:, 2], in_=w_view[:, 2])
        quantise_w(2)
        nc.vector.tensor_tensor(out=gbias[:], in0=gate[:], in1=bdf[:].unsqueeze(2).to_broadcast([P, 4, NA]),
                                op=ALU.mult)
        quantise_w(0)
        quantise_w(1)
        nc.vector.tensor_copy(out=f_grp[:], in_=f_raw[:].rearrange("p t f -> p f t"))
        evacuate(1)
        mask = const.tile([P, NA], F32, name="mask")
        nc.scalar.copy(out=mask[:], in_=m_bf[:])
        quantise(1)
        new_x(2)
        f_codes = const.tile([P, NF], U32, name="f_codes", align_bytes=64)
        f_scales = const.tile([P, NF], U8, name="f_scales", align_bytes=64)

        for s in range(2, NQ + 2):
            q1 = s - 2
            passes = PASSES[q1 % 3] if q1 < NQ - 2 else TAIL_PASSES
            st[("pl", q1)] = ring.tile([P, 2, 4 * W], BF16, name="planes", tag="ring", align_bytes=64)
            new_x(s + 1)
            if live(s - 3):
                regroup_gpsimd(s - 3)
            mx1(q1, passes[0][0])
            if live(s - 6):
                mx2(s - 6, (2, 3))
            mx1(q1, passes[1][0])
            if live(s):
                transposes(s)
            if live(s - 7):
                add_up(s - 7)
            if live(s + LOADS_AHEAD):
                load(s + LOADS_AHEAD)
            if live(s - 6):
                tanh(s - 6)
            if live(s):
                evacuate(s)
            if live(q1):
                for c, eng in passes[2:4]:
                    mx1(q1, c)
            if live(s - 5):
                mx2(s - 5, (0, 1))
            for c, eng in passes:
                if eng == "s":
                    gate_scalar(q1, c)
            vec = [c for c, eng in passes if eng == "v"]
            for c in vec:
                gate_vector(q1, c)
            if live(s - 3):
                regroup(s - 3)
            quantise(s)
            if s == 3:
                nc.vector.quantize_mx(out=f_codes[:].bitcast(FP8X4), scales=f_scales[:],
                                      in_=f_grp[:].rearrange("p f t -> p (f t)"))

        last = NQ - 1
        HW = W // 2
        halves = []
        for h in range(2):
            halves.append((const.tile([P, HW, 4], BF16, name=f"g_half{h}", align_bytes=64),
                           const.tile([P, HW], U32, name=f"c_half{h}", align_bytes=64),
                           const.tile([P, HW], U8, name=f"s_half{h}", align_bytes=64)))

        def regroup_half(h, copy):
            copy(out=halves[h][0][:].rearrange("p (x y) t -> p x t y", y=4),
                 in_=planes(last)[:, :, h * HW:(h + 1) * HW].rearrange("p t (x y) -> p x t y", y=4))

        mx2(last - 3, (2, 3))
        mx2(last - 2, range(QJ), tail=True)
        regroup_half(0, nc.vector.tensor_copy)
        tanh(last - 3)
        regroup_half(1, nc.scalar.copy)
        tanh(last - 2)
        quantise(last + 3)
        for h in range(2):
            nc.vector.quantize_mx(out=halves[h][1][:].bitcast(FP8X4), scales=halves[h][2][:],
                                  in_=halves[h][0][:].rearrange("p w t -> p (w t)"))
        add_up(last - 4)
        add_up(last - 3)
        mx2(last - 1, range(QJ), tail=True)
        tanh(last - 1)
        p2 = ps_1.tile([P, QJ, NF], F32, name="p2_last", tag="p1")
        for a in range(QJ):
            mx2_one(p2, a, halves[a // 2][1], halves[a // 2][2], a % 2)
        st[("p2", last)] = p2
        tanh(last)
        add_up(last - 2)
        add_up(last - 1)
        add_up(last)

        sumT = const.tile([P, NA], F32, name="sumT")
        nc.vector.tensor_copy(out=sumT[:], in_=accT[:])
        res_ps = ps_t.tile([P, NF], F32, name="res_ps", tag="tp")
        nc.tensor.transpose(res_ps[:], sumT[:], ident[:])
        res = const.tile([P, NF], F32, name="res")
        nc.vector.tensor_copy(out=res[:], in_=res_ps[:])
        nc.sync.dma_start(out=o_dram, in_=res[:])
